import numpy as np
import ml_dtypes


def mxq(x, axis, fmt="e4m3"):
    dtype, down = {"e4m3": (ml_dtypes.float8_e4m3fn, 7), "e5m2": (ml_dtypes.float8_e5m2, 14)}[fmt]
    v = np.moveaxis(np.asarray(x, np.float32).astype(ml_dtypes.bfloat16).astype(np.float64), axis, -1)
    blocks = v.reshape(v.shape[:-1] + (-1, 32))
    amax = np.abs(blocks).max(-1, keepdims=True)
    byte = np.maximum(np.where(amax > 0, np.frexp(amax)[1] - 1 + 127, 0) - down, 1)
    scale = np.exp2(byte - 127.0)
    codes = (blocks / scale).astype(np.float32).astype(dtype).astype(np.float64)
    return np.moveaxis((codes * scale).reshape(v.shape), -1, axis)


WIDE = False


def mx_kscale(k):
    if not WIDE:
        return np.ones(k)
    levels = np.array([10, -10, 5, -5, 0])
    a = np.random.permutation(np.resize(levels, k // 512 * 4)).reshape(k // 512, 4)
    idx = np.arange(k)
    return np.exp2(a[idx // 512, idx % 128 // 32])


BF16 = ml_dtypes.bfloat16


def bf(x):
    return np.asarray(x, np.float32).astype(BF16)


def f64(x):
    return np.asarray(x).astype(np.float64)


B, N, D, F = 4, 32, 512, 512


def setup_inputs():
    s, t = mx_kscale(D), mx_kscale(D)
    sst = np.concatenate([s, s, t])
    return {
        'node_h': bf(np.random.standard_normal((B, N, D)) * 0.5 * s),
        'rel_h': bf(np.random.standard_normal((B, N, N, D)) * 0.6 * t),
        'W_go': bf(np.random.standard_normal((D, D)) / np.sqrt(D) / s[:, None]),
        'b_go': bf(np.random.standard_normal(D) * 0.3),
        'W_gr': bf(np.random.standard_normal((3 * D, D)) * 1.5 / np.sqrt(3 * D) / sst[:, None]),
        'b_gr': bf(np.random.standard_normal(D) * 0.3),
        'W_esa': bf(np.random.standard_normal((D, F)) * 1.5 / np.sqrt(D)),
        'b_esa': bf(np.random.standard_normal(F) * 0.3),
    }


def reference(node_h, rel_h, W_go, b_go, W_gr, b_gr, W_esa, b_esa):
    xq = mxq(f64(node_h), 2, 'e4m3')
    wg = f64(W_gr)
    new_x = np.tanh((xq @ mxq(f64(W_go), 0, 'e4m3')) + f64(b_go))
    pre = ((xq @ mxq(wg[:D], 0, 'e4m3'))[:, :, None, :]
           + (xq @ mxq(wg[D:2 * D], 0, 'e4m3'))[:, None, :, :]
           + (mxq(f64(rel_h), 3, 'e4m3') @ mxq(wg[2 * D:], 0, 'e4m3')) + f64(b_gr))
    rel = np.tanh(pre)
    e = (mxq(rel, 3, 'e4m3') @ mxq(f64(W_esa), 0, 'e4m3')) + f64(b_esa)
    p = np.exp(e - e.max(axis=1, keepdims=True))
    attn = p / p.sum(axis=1, keepdims=True)
    return new_x, (attn * e).sum(axis=2)

@@ -1,0 +1,355 @@
+from contextlib import ExitStack
+
+import concourse.mybir as mybir
+from concourse.masks import make_identity
+
+F32 = mybir.dt.float32
+BF16 = mybir.dt.bfloat16
+U32 = mybir.dt.uint32
+U8 = mybir.dt.uint8
+I32 = mybir.dt.int32
+FP8X4 = mybir.dt.float8_e4m3fn_x4
+ACT = mybir.ActivationFunctionType
+ALU = mybir.AluOpType
+AX = mybir.AxisListType
+
+P = 128
+FLOPS = 2 * 512 * 512 * (3 * 128 + 2 * 4096)
+
+SHORT_CT = (0, 1)
+COPY_ENGINE = ("s", "s", "s", "s")
+WEIGHT_ENGINE = {"gc": "v", "ga": "s", "gb": "v", "we": "s", "go": "v"}
+
+
+def tile_languagemsgencoder_pb_kernel(
+    tc, node_h, rel_h, W_go, b_go, W_gr, b_gr, W_esa, b_esa, out_0, out_1
+):
+    nc = tc.nc
+    with ExitStack() as ctx:
+        const = ctx.enter_context(tc.tile_pool(name="const", bufs=1))
+        work = ctx.enter_context(tc.tile_pool(name="work", bufs=2))
+        psum = ctx.enter_context(tc.psum_pool(name="psum", bufs=2))
+
+        x_sb = const.tile([P, 512], BF16, name="x_sb")
+        nc.sync.dma_start(out=x_sb[:], in_=node_h.flatten_outer_dims())
+
+        braw = const.tile([P, P], BF16, name="braw")
+        nc.vector.memset(braw[:], 0.0)
+        nc.scalar.dma_start(out=braw[0:4, :], in_=b_gr.rearrange("(t p) -> t p", p=P))
+        nc.scalar.dma_start(out=braw[4:8, :], in_=b_esa.rearrange("(t p) -> t p", p=P))
+        nc.scalar.dma_start(out=braw[8:12, :], in_=b_go.rearrange("(t p) -> t p", p=P))
+
+        raw = {}
+
+        def load_weight(key, rows, pairs):
+            w_raw = const.tile([P, 4, 512], BF16, name="raw_" + key)
+            if pairs:
+                nc.sync.dma_start(
+                    out=w_raw[:].rearrange("p (u e) c -> p u (e c)", u=2),
+                    in_=rows.rearrange("(u q e) c -> q u (e c)", u=2, e=2),
+                )
+            else:
+                nc.sync.dma_start(out=w_raw[:], in_=rows.rearrange("(t p) c -> p t c", p=P))
+            raw[key] = w_raw
+
+        rel_rows = rel_h.rearrange("b i j k -> b (i j) k")
+        rel_raw = []
+        for b in range(4):
+            rel_b = const.tile([P, 8, 512], BF16, name="rel_raw%d" % b)
+            rel_raw.append(rel_b)
+
+        def load_rel(b, h):
+            nc.sync.dma_start(
+                out=rel_raw[b][:, 4 * h : 4 * h + 4, :],
+                in_=rel_rows[b].rearrange("(p g) k -> p g k", g=8)[:, 4 * h : 4 * h + 4, :],
+            )
+
+        load_weight("gc", W_gr[1024:1536, :], True)
+        load_rel(0, 0)
+        load_weight("ga", W_gr[0:512, :], True)
+        load_weight("gb", W_gr[512:1024, :], True)
+        load_weight("we", W_esa, False)
+        load_rel(0, 1)
+        load_weight("go", W_go, True)
+        for b in range(1, 4):
+            load_rel(b, 0)
+            load_rel(b, 1)
+
+        ident = const.tile([P, P], F32, name="ident")
+        make_identity(nc, ident[:])
+        fold = const.tile([P, 32], F32, name="fold")
+        nc.vector.tensor_reduce(
+            out=fold[:], in_=ident[:].rearrange("p (a i) -> p i a", a=4), axis=AX.X, op=ALU.add
+        )
+        sel = const.tile([P, 4, P], F32, name="sel")
+        nc.vector.memset(sel[:], 0.0)
+        for b in range(4):
+            nc.vector.tensor_copy(out=sel[:, b, 32 * b : 32 * b + 32], in_=fold[:])
+
+        xw = x_sb[:].bitcast(F32)
+        xt = psum.tile([P, 2, 2, P], F32, name="xt", tag="tp")
+        for u in range(2):
+            nc.tensor.transpose(xt[:, 0, u, :], xw[:, 128 * u : 128 * u + 128], ident[:])
+        xg = const.tile([P, P, 2], F32, name="xg", align_bytes=64)
+        nc.vector.tensor_copy(out=xg[:], in_=xt[:, 0, :, :].rearrange("p u c -> p c u"))
+        x4 = const.tile([P, P, 4, 2], F32, name="x4", align_bytes=64)
+        nc.vector.tensor_copy(out=x4[:], in_=xg[:].unsqueeze(2).to_broadcast([P, P, 4, 2]))
+
+        xc = const.tile([P, P], U32, name="xc", align_bytes=64)
+        xs = const.tile([P, P], U8, name="xs", align_bytes=64)
+        x4c = const.tile([P, 512], U32, name="x4c", align_bytes=64)
+        x4s = const.tile([P, 512], U8, name="x4s", align_bytes=64)
+        nc.vector.memset(xs[:].bitcast(I32), 0)
+        nc.vector.memset(x4s[:].bitcast(I32), 0)
+        nc.vector.quantize_mx(
+            out=xc[:].bitcast(FP8X4),
+            scales=xs[:],
+            in_=xg[:].rearrange("p c u -> p (c u)").bitcast(BF16),
+        )
+        nc.vector.quantize_mx(
+            out=x4c[:].bitcast(FP8X4),
+            scales=x4s[:],
+            in_=x4[:].rearrange("p c r u -> p (c r u)").bitcast(BF16),
+        )
+
+        bf = const.tile([P, P], F32, name="bf")
+        nc.vector.tensor_copy(out=bf[:], in_=braw[:])
+        bt = psum.tile([P, 512], F32, name="bt", tag="tp")
+        nc.tensor.transpose(bt[:, 0:P], bf[:], ident[:])
+        bias = const.tile([P, 12], F32, name="bias")
+        nc.vector.tensor_copy(out=bias[:], in_=bt[:, 0:12])
+
+        wc = {}
+        ws = {}
+
+        def prep_weight(key):
+            grouped = work.tile([P, 512, 4], BF16, name="wg", tag="wg", align_bytes=64)
+            dst = grouped[:].rearrange("p (c i) t -> p c t i", i=4)
+            src = raw[key][:].rearrange("p t (c i) -> p c t i", i=4)
+            if WEIGHT_ENGINE[key] == "v":
+                nc.vector.tensor_copy(out=dst, in_=src)
+            else:
+                nc.scalar.copy(out=dst, in_=src)
+            codes = const.tile([P, 512], U32, name="c_" + key, align_bytes=64)
+            scales = const.tile([P, 512], U8, name="s_" + key, align_bytes=64)
+            nc.vector.quantize_mx(
+                out=codes[:].bitcast(FP8X4),
+                scales=scales[:],
+                in_=grouped[:].rearrange("p c t -> p (c t)"),
+            )
+            wc[key] = codes
+            ws[key] = scales
+
+        for key in ("gc", "ga", "gb", "we"):
+            prep_weight(key)
+
+        a_codes = []
+        a_scales = []
+        for b in range(4):
+            ac = const.tile([P, 512], U32, name="ac%d" % b, align_bytes=64)
+            asc = const.tile([P, 512], U8, name="as%d" % b, align_bytes=64)
+            nc.vector.tensor_copy(
+                out=ac[:].bitcast(I32).rearrange("p (r c) -> p r c", r=16),
+                in_=xc[:, 32 * b : 32 * b + 32].bitcast(I32).unsqueeze(1).to_broadcast([P, 16, 32]),
+            )
+            nc.vector.tensor_copy(
+                out=asc[:].bitcast(I32).rearrange("p (r c) -> p r c", r=16),
+                in_=xs[:, 32 * b : 32 * b + 32].bitcast(I32).unsqueeze(1).to_broadcast([P, 16, 8]),
+            )
+            a_codes.append(ac)
+            a_scales.append(asc)
+
+        def mx(out, key, t, rhs, rhs_scale, start, stop):
+            nc.tensor.matmul_mx(
+                out=out,
+                lhsT=wc[key][:, 128 * t : 128 * t + 128].bitcast(FP8X4),
+                lhsT_scale=ws[key][:, 128 * t : 128 * t + 128],
+                rhs=rhs.bitcast(FP8X4),
+                rhs_scale=rhs_scale,
+                start=start,
+                stop=stop,
+            )
+
+        def front(n):
+            b, h = divmod(n, 2)
+            relw = rel_raw[b][:].rearrange("p g k -> p (g k)").bitcast(F32)
+            hg = work.tile([P, 512, 2], F32, name="hg", tag="hg", align_bytes=64)
+            for gp in range(2):
+                tp = psum.tile([P, 2, 2, P], F32, name="tp", tag="tp")
+                for q in range(2):
+                    g = 4 * h + 2 * gp + q
+                    for u in range(2):
+                        lo = 256 * g + 128 * u
+                        nc.tensor.transpose(tp[:, q, u, :], relw[:, lo : lo + 128], ident[:])
+                for q in range(2):
+                    gl = 2 * gp + q
+                    dst = hg[:, 128 * gl : 128 * gl + 128, :].rearrange("p (a i) u -> p a i u", a=4)
+                    src = tp[:, q, :, :].rearrange("p u (i a) -> p a i u", a=4)
+                    if COPY_ENGINE[gl] == "s":
+                        nc.scalar.copy(out=dst, in_=src)
+                    else:
+                        nc.vector.tensor_copy(out=dst, in_=src)
+            hc = work.tile([P, 512], U32, name="hc", tag="hc", align_bytes=64)
+            hs = work.tile([P, 512], U8, name="hs", tag="hs", align_bytes=64)
+            nc.vector.quantize_mx(
+                out=hc[:].bitcast(FP8X4),
+                scales=hs[:],
+                in_=hg[:].rearrange("p c u -> p (c u)").bitcast(BF16),
+            )
+            bc = work.tile([P, 512], U32, name="bc", tag="bc", align_bytes=64)
+            bs = work.tile([P, 512], U8, name="bs", tag="bs", align_bytes=64)
+            tok = slice(32 * b, 32 * b + 32)
+            nc.vector.tensor_copy(
+                out=bc[:].bitcast(I32).rearrange("p (g a i) -> p g a i", g=4, a=4),
+                in_=xc[:, tok]
+                .bitcast(I32)
+                .rearrange("p (a h g) -> p h g a", a=4, h=2)[:, h, :, :]
+                .unsqueeze(3)
+                .to_broadcast([P, 4, 4, 32]),
+            )
+            nc.vector.tensor_copy(
+                out=bs[:].bitcast(I32).rearrange("p (g a w) -> p g a w", g=4, a=4),
+                in_=x4s[:]
+                .bitcast(I32)[:, tok]
+                .rearrange("p (a h g) -> p h g a", a=4, h=2)[:, h, :, :]
+                .unsqueeze(3)
+                .to_broadcast([P, 4, 4, 8]),
+            )
+            return hc, hs, bc, bs
+
+        def stage1(n, ops):
+            b = n // 2
+            hc, hs, bc, bs = ops
+            rt = work.tile([P, 4, 512], BF16, name="rt", tag="rt")
+            for t in range(4):
+                s1 = psum.tile([P, 512], F32, name="s1", tag="s1")
+                mx(s1[:], "gc", t, hc[:], hs[:], True, False)
+                mx(s1[:], "ga", t, a_codes[b][:], a_scales[b][:], False, False)
+                mx(s1[:], "gb", t, bc[:], bs[:], False, True)
+                nc.scalar.activation(
+                    out=rt[:, t, :], in_=s1[:], func=ACT.Tanh, bias=bias[:, t : t + 1], scale=1.0
+                )
+            rg = work.tile([P, 512, 4], BF16, name="rg", tag="rg", align_bytes=64)
+            nc.vector.tensor_copy(
+                out=rg[:].rearrange("p (c i) t -> p c t i", i=4),
+                in_=rt[:].rearrange("p t (c i) -> p c t i", i=4),
+            )
+            rc = work.tile([P, 512], U32, name="rc", tag="rc", align_bytes=64)
+            rs = work.tile([P, 512], U8, name="rs", tag="rs", align_bytes=64)
+            nc.vector.quantize_mx(
+                out=rc[:].bitcast(FP8X4), scales=rs[:], in_=rg[:].rearrange("p c t -> p (c t)")
+            )
+            return rc, rs
+
+        u_tiles = {}
+
+        def stage2(n, rel_ops):
+            h = n % 2
+            rc, rs = rel_ops
+            for ct in range(4):
+                e = psum.tile([P, 512], F32, name="e", tag="e")
+                mx(e[:], "we", ct, rc[:], rs[:], True, True)
+                e3 = e[:].rearrange("p (j i) -> p j i", i=32)
+                negm = work.tile([P, 16], F32, name="negm", tag="negm", bufs=3)
+                nc.vector.tensor_reduce(out=negm[:], in_=e3, axis=AX.X, op=ALU.max, negate=True)
+                pr = work.tile([P, 16, 32], F32, name="pr", tag="pr", bufs=3)
+                if ct in SHORT_CT:
+                    z = work.tile([P, 16], F32, name="zs", tag="zs", bufs=3)
+                    for j in range(16):
+                        nc.scalar.activation(
+                            out=pr[:, j, :],
+                            in_=e3[:, j, :],
+                            func=ACT.Exp,
+                            bias=negm[:, j : j + 1],
+                            scale=1.0,
+                            accum_out=z[:, j : j + 1],
+                        )
+                else:
+                    z = work.tile([P, 16], F32, name="zv", tag="zv", bufs=3)
+                    d = work.tile([P, 16, 32], F32, name="d", tag="d", bufs=2)
+                    nc.vector.tensor_tensor(
+                        out=d[:],
+                        in0=e3,
+                        in1=negm[:].unsqueeze(2).to_broadcast([P, 16, 32]),
+                        op=ALU.add,
+                    )
+                    nc.scalar.activation(out=pr[:], in_=d[:], func=ACT.Exp)
+                    nc.vector.tensor_reduce(out=z[:], in_=pr[:], axis=AX.X, op=ALU.add)
+                rz = work.tile([P, 16], F32, name="rz", tag="rz", bufs=3)
+                nc.vector.reciprocal(out=rz[:], in_=z[:])
+                y = work.tile([P, 16, 32], F32, name="y", tag="y", bufs=3)
+                nc.vector.scalar_tensor_tensor(
+                    out=y[:].rearrange("p j i -> p (j i)"),
+                    in0=e[:],
+                    scalar=bias[:, 4 + ct : 5 + ct],
+                    in1=pr[:].rearrange("p j i -> p (j i)"),
+                    op0=ALU.add,
+                    op1=ALU.mult,
+                )
+                u = work.tile([P, 16, 32], F32, name="u", tag="u", bufs=12)
+                nc.gpsimd.tensor_tensor(
+                    out=u[:],
+                    in0=y[:],
+                    in1=rz[:].unsqueeze(2).to_broadcast([P, 16, 32]),
+                    op=ALU.mult,
+                )
+                u_tiles[(h, ct)] = u
+
+        r_ps = psum.tile([P, 512], F32, name="r_ps", tag="r", bufs=1)
+
+        def batch_end(b):
+            acc = psum.tile([P, 512], F32, name="acc", tag="acc", bufs=1)
+            for ct in range(4):
+                for k in range(8):
+                    h, q = divmod(k, 4)
+                    nc.tensor.matmul(
+                        out=acc[:, 128 * ct : 128 * ct + 128],
+                        lhsT=u_tiles[(h, ct)][:].rearrange("p j i -> p (j i)")[
+                            :, 128 * q : 128 * q + 128
+                        ],
+                        rhs=ident[:],
+                        start=(k == 0),
+                        stop=(k == 7),
+                        is_transpose=True,
+                    )
+            accs = work.tile([P, 512], F32, name="accs", tag="accs")
+            nc.scalar.copy(out=accs[:], in_=acc[:])
+            nc.tensor.matmul(
+                out=r_ps[:], lhsT=sel[:, b, :], rhs=accs[:], start=(b == 0), stop=(b == 3)
+            )
+
+        def new_x():
+            prep_weight("go")
+            nxp = psum.tile([P, 4, P], F32, name="nxp", tag="s1")
+            nxt = const.tile([P, 4, P], F32, name="nxt")
+            for t in range(4):
+                mx(nxp[:, t, :], "go", t, xc[:], xs[:], True, True)
+            for t in range(4):
+                nc.scalar.activation(
+                    out=nxt[:, t, :],
+                    in_=nxp[:, t, :],
+                    func=ACT.Tanh,
+                    bias=bias[:, 8 + t : 9 + t],
+                    scale=1.0,
+                )
+            nxo_ps = psum.tile([P, 512], F32, name="nxo_ps", tag="tp")
+            for t in range(4):
+                nc.tensor.transpose(nxo_ps[:, 128 * t : 128 * t + 128], nxt[:, t, :], ident[:])
+            nxo = const.tile([P, 512], F32, name="nxo")
+            nc.scalar.copy(out=nxo[:], in_=nxo_ps[:])
+            nc.sync.dma_start(out=out_0.flatten_outer_dims(), in_=nxo[:])
+
+        ops = front(0)
+        for n in range(8):
+            nxt_ops = front(n + 1) if n < 7 else None
+            rel_ops = stage1(n, ops)
+            stage2(n, rel_ops)
+            if n % 2 == 1:
+                batch_end(n // 2)
+            if n == 2:
+                new_x()
+            ops = nxt_ops
+
+        ro = const.tile([P, 512], F32, name="ro")
+        nc.vector.tensor_copy(out=ro[:], in_=r_ps[:])
+        nc.sync.dma_start(out=out_1.flatten_outer_dims(), in_=ro[:])

@@ -16,9 +16,22 @@ AX = mybir.AxisListType
 P = 128
 FLOPS = 2 * 512 * 512 * (3 * 128 + 2 * 4096)
 
-SHORT_CT = (0, 1)
-COPY_ENGINE = ("s", "s", "s", "s")
-WEIGHT_ENGINE = {"gc": "v", "ga": "s", "gb": "v", "we": "s", "go": "v"}
+N_BANKS = 32
+LONG_BANK = 3
+AHEAD_MAX = 2
+AHEAD_EXP = 1
+AHEAD_STAGE1 = 8
+AHEAD_QUANT_REL = 6
+AHEAD_QUANT_H = 16
+AHEAD_TRANSPOSE = 17
+BEHIND_SUM = 3
+BEHIND_FOLD = 5
+
+
+def bank_at(x):
+    if 0 <= x < N_BANKS:
+        return divmod(x, 4)
+    return None
 
 
 def tile_languagemsgencoder_pb_kernel(
@@ -29,15 +42,16 @@ def tile_languagemsgencoder_pb_kernel(
         const = ctx.enter_context(tc.tile_pool(name="const", bufs=1))
         work = ctx.enter_context(tc.tile_pool(name="work", bufs=2))
         psum = ctx.enter_context(tc.psum_pool(name="psum", bufs=2))
-
-        x_sb = const.tile([P, 512], BF16, name="x_sb")
-        nc.sync.dma_start(out=x_sb[:], in_=node_h.flatten_outer_dims())
+        ctx.enter_context(tc.manual_schedule())
 
         braw = const.tile([P, P], BF16, name="braw")
         nc.vector.memset(braw[:], 0.0)
         nc.scalar.dma_start(out=braw[0:4, :], in_=b_gr.rearrange("(t p) -> t p", p=P))
         nc.scalar.dma_start(out=braw[4:8, :], in_=b_esa.rearrange("(t p) -> t p", p=P))
         nc.scalar.dma_start(out=braw[8:12, :], in_=b_go.rearrange("(t p) -> t p", p=P))
+
+        x_sb = const.tile([P, 512], BF16, name="x_sb")
+        nc.sync.dma_start(out=x_sb[:], in_=node_h.flatten_outer_dims())
 
         raw = {}
 
@@ -58,42 +72,36 @@ def tile_languagemsgencoder_pb_kernel(
             rel_b = const.tile([P, 8, 512], BF16, name="rel_raw%d" % b)
             rel_raw.append(rel_b)
 
-        def load_rel(b, h):
+        def load_rel(k):
+            b, h = divmod(k, 2)
             nc.sync.dma_start(
                 out=rel_raw[b][:, 4 * h : 4 * h + 4, :],
                 in_=rel_rows[b].rearrange("(p g) k -> p g k", g=8)[:, 4 * h : 4 * h + 4, :],
             )
 
         load_weight("gc", W_gr[1024:1536, :], True)
-        load_rel(0, 0)
         load_weight("ga", W_gr[0:512, :], True)
+        load_rel(0)
         load_weight("gb", W_gr[512:1024, :], True)
         load_weight("we", W_esa, False)
-        load_rel(0, 1)
+        for k in range(1, 8):
+            load_rel(k)
         load_weight("go", W_go, True)
-        for b in range(1, 4):
-            load_rel(b, 0)
-            load_rel(b, 1)
 
         ident = const.tile([P, P], F32, name="ident")
         make_identity(nc, ident[:])
-        fold = const.tile([P, 32], F32, name="fold")
-        nc.vector.tensor_reduce(
-            out=fold[:], in_=ident[:].rearrange("p (a i) -> p i a", a=4), axis=AX.X, op=ALU.add
-        )
+        bf = const.tile([P, P], F32, name="bf")
+        nc.gpsimd.tensor_copy(out=bf[:], in_=braw[:])
         sel = const.tile([P, 4, P], F32, name="sel")
-        nc.vector.memset(sel[:], 0.0)
+        nc.gpsimd.memset(sel[:], 0.0)
+        fold_a = const.tile([P, 32], F32, name="fold_a")
+        fold_b = const.tile([P, 32], F32, name="fold_b")
+        nc.gpsimd.tensor_tensor(out=fold_a[:], in0=ident[:, 0:32], in1=ident[:, 32:64], op=ALU.add)
+        nc.gpsimd.tensor_tensor(out=fold_b[:], in0=ident[:, 64:96], in1=ident[:, 96:128], op=ALU.add)
         for b in range(4):
-            nc.vector.tensor_copy(out=sel[:, b, 32 * b : 32 * b + 32], in_=fold[:])
-
-        xw = x_sb[:].bitcast(F32)
-        xt = psum.tile([P, 2, 2, P], F32, name="xt", tag="tp")
-        for u in range(2):
-            nc.tensor.transpose(xt[:, 0, u, :], xw[:, 128 * u : 128 * u + 128], ident[:])
-        xg = const.tile([P, P, 2], F32, name="xg", align_bytes=64)
-        nc.vector.tensor_copy(out=xg[:], in_=xt[:, 0, :, :].rearrange("p u c -> p c u"))
-        x4 = const.tile([P, P, 4, 2], F32, name="x4", align_bytes=64)
-        nc.vector.tensor_copy(out=x4[:], in_=xg[:].unsqueeze(2).to_broadcast([P, P, 4, 2]))
+            nc.gpsimd.tensor_tensor(
+                out=sel[:, b, 32 * b : 32 * b + 32], in0=fold_a[:], in1=fold_b[:], op=ALU.add
+            )
 
         xc = const.tile([P, P], U32, name="xc", align_bytes=64)
         xs = const.tile([P, P], U8, name="xs", align_bytes=64)
@@ -101,51 +109,64 @@ def tile_languagemsgencoder_pb_kernel(
         x4s = const.tile([P, 512], U8, name="x4s", align_bytes=64)
         nc.vector.memset(xs[:].bitcast(I32), 0)
         nc.vector.memset(x4s[:].bitcast(I32), 0)
+
+        xw = x_sb[:].bitcast(F32)
+        xt = psum.tile([P, 2, 2, P], F32, name="xt", tag="tp")
+        for u in range(2):
+            nc.tensor.transpose(xt[:, 0, u, :], xw[:, 128 * u : 128 * u + 128], ident[:])
+        bt = psum.tile([P, 512], F32, name="bt", tag="tp")
+        nc.tensor.transpose(bt[:, 0:P], bf[:], ident[:])
+        xg = const.tile([P, P, 2], F32, name="xg", align_bytes=64)
+        nc.vector.tensor_copy(out=xg[:], in_=xt[:, 0, :, :].rearrange("p u c -> p c u"))
+        x4 = const.tile([P, P, 4, 2], F32, name="x4", align_bytes=64)
+        nc.scalar.copy(out=x4[:], in_=xg[:].unsqueeze(2).to_broadcast([P, P, 4, 2]))
+        bias = const.tile([P, 12], F32, name="bias")
+        nc.scalar.copy(out=bias[:], in_=bt[:, 0:12])
         nc.vector.quantize_mx(
             out=xc[:].bitcast(FP8X4),
             scales=xs[:],
             in_=xg[:].rearrange("p c u -> p (c u)").bitcast(BF16),
         )
-        nc.vector.quantize_mx(
-            out=x4c[:].bitcast(FP8X4),
-            scales=x4s[:],
-            in_=x4[:].rearrange("p c r u -> p (c r u)").bitcast(BF16),
-        )
-
-        bf = const.tile([P, P], F32, name="bf")
-        nc.vector.tensor_copy(out=bf[:], in_=braw[:])
-        bt = psum.tile([P, 512], F32, name="bt", tag="tp")
-        nc.tensor.transpose(bt[:, 0:P], bf[:], ident[:])
-        bias = const.tile([P, 12], F32, name="bias")
-        nc.vector.tensor_copy(out=bias[:], in_=bt[:, 0:12])
 
         wc = {}
         ws = {}
+        wg = {}
 
-        def prep_weight(key):
-            grouped = work.tile([P, 512, 4], BF16, name="wg", tag="wg", align_bytes=64)
-            dst = grouped[:].rearrange("p (c i) t -> p c t i", i=4)
-            src = raw[key][:].rearrange("p t (c i) -> p c t i", i=4)
-            if WEIGHT_ENGINE[key] == "v":
-                nc.vector.tensor_copy(out=dst, in_=src)
+        def regroup_weight(key, engine):
+            grouped = const.tile([P, 512, 4], BF16, name="wg_" + key, align_bytes=64)
+            if engine == "g":
+                nc.gpsimd.tensor_scalar(
+                    out=grouped[:],
+                    in0=raw[key][:].rearrange("p t c -> p c t"),
+                    scalar1=1.0,
+                    scalar2=0.0,
+                    op0=ALU.mult,
+                    op1=ALU.add,
+                )
             else:
-                nc.scalar.copy(out=dst, in_=src)
+                dst = grouped[:].rearrange("p (c i) t -> p c t i", i=4)
+                src = raw[key][:].rearrange("p t (c i) -> p c t i", i=4)
+                if engine == "v":
+                    nc.vector.tensor_copy(out=dst, in_=src)
+                else:
+                    nc.scalar.copy(out=dst, in_=src)
+            wg[key] = grouped
+
+        def quantise_weight(key):
             codes = const.tile([P, 512], U32, name="c_" + key, align_bytes=64)
             scales = const.tile([P, 512], U8, name="s_" + key, align_bytes=64)
             nc.vector.quantize_mx(
                 out=codes[:].bitcast(FP8X4),
                 scales=scales[:],
-                in_=grouped[:].rearrange("p c t -> p (c t)"),
+                in_=wg[key][:].rearrange("p c t -> p (c t)"),
             )
             wc[key] = codes
             ws[key] = scales
 
-        for key in ("gc", "ga", "gb", "we"):
-            prep_weight(key)
+        a_codes = {}
+        a_scales = {}
 
-        a_codes = []
-        a_scales = []
-        for b in range(4):
+        def spread_xi(b):
             ac = const.tile([P, 512], U32, name="ac%d" % b, align_bytes=64)
             asc = const.tile([P, 512], U8, name="as%d" % b, align_bytes=64)
             nc.vector.tensor_copy(
@@ -156,8 +177,23 @@ def tile_languagemsgencoder_pb_kernel(
                 out=asc[:].bitcast(I32).rearrange("p (r c) -> p r c", r=16),
                 in_=xs[:, 32 * b : 32 * b + 32].bitcast(I32).unsqueeze(1).to_broadcast([P, 16, 8]),
             )
-            a_codes.append(ac)
-            a_scales.append(asc)
+            a_codes[b] = ac
+            a_scales[b] = asc
+
+        regroup_weight("gc", "v")
+        quantise_weight("gc")
+        regroup_weight("ga", "s")
+        nc.vector.quantize_mx(
+            out=x4c[:].bitcast(FP8X4),
+            scales=x4s[:],
+            in_=x4[:].rearrange("p c r u -> p (c r u)").bitcast(BF16),
+        )
+        spread_xi(0)
+        regroup_weight("gb", "v")
+        quantise_weight("ga")
+        quantise_weight("gb")
+        regroup_weight("we", "g")
+        regroup_weight("go", "g")
 
         def mx(out, key, t, rhs, rhs_scale, start, stop):
             nc.tensor.matmul_mx(
@@ -170,34 +206,46 @@ def tile_languagemsgencoder_pb_kernel(
                 stop=stop,
             )
 
-        def front(n):
-            b, h = divmod(n, 2)
+        st = {}
+
+        def transpose_half(k, gp):
+            b, h = divmod(k, 2)
             relw = rel_raw[b][:].rearrange("p g k -> p (g k)").bitcast(F32)
-            hg = work.tile([P, 512, 2], F32, name="hg", tag="hg", align_bytes=64)
-            for gp in range(2):
-                tp = psum.tile([P, 2, 2, P], F32, name="tp", tag="tp")
-                for q in range(2):
-                    g = 4 * h + 2 * gp + q
-                    for u in range(2):
-                        lo = 256 * g + 128 * u
-                        nc.tensor.transpose(tp[:, q, u, :], relw[:, lo : lo + 128], ident[:])
-                for q in range(2):
-                    gl = 2 * gp + q
-                    dst = hg[:, 128 * gl : 128 * gl + 128, :].rearrange("p (a i) u -> p a i u", a=4)
-                    src = tp[:, q, :, :].rearrange("p u (i a) -> p a i u", a=4)
-                    if COPY_ENGINE[gl] == "s":
-                        nc.scalar.copy(out=dst, in_=src)
-                    else:
-                        nc.vector.tensor_copy(out=dst, in_=src)
-            hc = work.tile([P, 512], U32, name="hc", tag="hc", align_bytes=64)
-            hs = work.tile([P, 512], U8, name="hs", tag="hs", align_bytes=64)
+            tp = psum.tile([P, 2, 2, P], F32, name="tp", tag="tp")
+            for q in range(2):
+                g = 4 * h + 2 * gp + q
+                for u in range(2):
+                    lo = 256 * g + 128 * u
+                    nc.tensor.transpose(tp[:, q, u, :], relw[:, lo : lo + 128], ident[:])
+            st[("tp", k, gp)] = tp
+
+        def copy_out(k, gl):
+            if gl == 0:
+                hg_new = work.tile([P, 512, 2], F32, name="hg", tag="hg", align_bytes=64)
+                st[("hg", k)] = hg_new
+            hg = st[("hg", k)]
+            gp, q = divmod(gl, 2)
+            dst = hg[:, 128 * gl : 128 * gl + 128, :].rearrange("p (a i) u -> p a i u", a=4)
+            src = st[("tp", k, gp)][:, q, :, :].rearrange("p u (i a) -> p a i u", a=4)
+            if gp == 0:
+                nc.scalar.copy(out=dst, in_=src)
+            else:
+                nc.vector.tensor_copy(out=dst, in_=src)
+
+        def quantise_h(k):
+            hc = work.tile([P, 512], U32, name="hc", tag="hc", bufs=4, align_bytes=64)
+            hs = work.tile([P, 512], U8, name="hs", tag="hs", bufs=4, align_bytes=64)
             nc.vector.quantize_mx(
                 out=hc[:].bitcast(FP8X4),
                 scales=hs[:],
-                in_=hg[:].rearrange("p c u -> p (c u)").bitcast(BF16),
+                in_=st[("hg", k)][:].rearrange("p c u -> p (c u)").bitcast(BF16),
             )
-            bc = work.tile([P, 512], U32, name="bc", tag="bc", align_bytes=64)
-            bs = work.tile([P, 512], U8, name="bs", tag="bs", align_bytes=64)
+            st[("h", k)] = (hc, hs)
+
+        def spread_xj(k):
+            b, h = divmod(k, 2)
+            bc = work.tile([P, 512], U32, name="bc", tag="bc", bufs=4, align_bytes=64)
+            bs = work.tile([P, 512], U8, name="bs", tag="bs", bufs=4, align_bytes=64)
             tok = slice(32 * b, 32 * b + 32)
             nc.vector.tensor_copy(
                 out=bc[:].bitcast(I32).rearrange("p (g a i) -> p g a i", g=4, a=4),
@@ -215,140 +263,223 @@ def tile_languagemsgencoder_pb_kernel(
                 .unsqueeze(3)
                 .to_broadcast([P, 4, 4, 8]),
             )
-            return hc, hs, bc, bs
+            st[("xj", k)] = (bc, bs)
 
-        def stage1(n, ops):
-            b = n // 2
-            hc, hs, bc, bs = ops
-            rt = work.tile([P, 4, 512], BF16, name="rt", tag="rt")
-            for t in range(4):
-                s1 = psum.tile([P, 512], F32, name="s1", tag="s1")
-                mx(s1[:], "gc", t, hc[:], hs[:], True, False)
-                mx(s1[:], "ga", t, a_codes[b][:], a_scales[b][:], False, False)
-                mx(s1[:], "gb", t, bc[:], bs[:], False, True)
-                nc.scalar.activation(
-                    out=rt[:, t, :], in_=s1[:], func=ACT.Tanh, bias=bias[:, t : t + 1], scale=1.0
-                )
-            rg = work.tile([P, 512, 4], BF16, name="rg", tag="rg", align_bytes=64)
-            nc.vector.tensor_copy(
-                out=rg[:].rearrange("p (c i) t -> p c t i", i=4),
-                in_=rt[:].rearrange("p t (c i) -> p c t i", i=4),
+        def stage1_mm(k, t):
+            hc, hs = st[("h", k)]
+            bc, bs = st[("xj", k)]
+            s1 = psum.tile([P, 512], F32, name="s1", tag="s1")
+            mx(s1[:], "gc", t, hc[:], hs[:], True, False)
+            mx(s1[:], "ga", t, a_codes[k // 2][:], a_scales[k // 2][:], False, False)
+            mx(s1[:], "gb", t, bc[:], bs[:], False, True)
+            st[("s1", k, t)] = s1
+
+        def stage1_tanh(k, t):
+            if t == 0:
+                rt_new = work.tile([P, 4, 512], BF16, name="rt", tag="rt")
+                st[("rt", k)] = rt_new
+            nc.scalar.activation(
+                out=st[("rt", k)][:, t, :],
+                in_=st[("s1", k, t)][:],
+                func=ACT.Tanh,
+                bias=bias[:, t : t + 1],
+                scale=1.0,
             )
+
+        def regroup_rel(k):
+            rt = st[("rt", k)]
+            rg = work.tile([P, 512, 4], BF16, name="rg", tag="rg", align_bytes=64)
+            if k == 0:
+                nc.vector.tensor_copy(
+                    out=rg[:].rearrange("p (c i) t -> p c t i", i=4),
+                    in_=rt[:].rearrange("p t (c i) -> p c t i", i=4),
+                )
+            else:
+                nc.gpsimd.tensor_scalar(
+                    out=rg[:],
+                    in0=rt[:].rearrange("p t c -> p c t"),
+                    scalar1=1.0,
+                    scalar2=0.0,
+                    op0=ALU.mult,
+                    op1=ALU.add,
+                )
+            st[("rg", k)] = rg
+
+        def quantise_rel(k):
             rc = work.tile([P, 512], U32, name="rc", tag="rc", align_bytes=64)
             rs = work.tile([P, 512], U8, name="rs", tag="rs", align_bytes=64)
             nc.vector.quantize_mx(
-                out=rc[:].bitcast(FP8X4), scales=rs[:], in_=rg[:].rearrange("p c t -> p (c t)")
+                out=rc[:].bitcast(FP8X4),
+                scales=rs[:],
+                in_=st[("rg", k)][:].rearrange("p c t -> p (c t)"),
             )
-            return rc, rs
+            st[("r", k)] = (rc, rs)
 
-        u_tiles = {}
+        def stage2_mm(k, ct):
+            rc, rs = st[("r", k)]
+            e = psum.tile([P, 512], F32, name="e", tag="e", bufs=3)
+            mx(e[:], "we", ct, rc[:], rs[:], True, True)
+            st[("e", k, ct)] = e
 
-        def stage2(n, rel_ops):
-            h = n % 2
-            rc, rs = rel_ops
-            for ct in range(4):
-                e = psum.tile([P, 512], F32, name="e", tag="e")
-                mx(e[:], "we", ct, rc[:], rs[:], True, True)
-                e3 = e[:].rearrange("p (j i) -> p j i", i=32)
-                negm = work.tile([P, 16], F32, name="negm", tag="negm", bufs=3)
-                nc.vector.tensor_reduce(out=negm[:], in_=e3, axis=AX.X, op=ALU.max, negate=True)
-                pr = work.tile([P, 16, 32], F32, name="pr", tag="pr", bufs=3)
-                if ct in SHORT_CT:
-                    z = work.tile([P, 16], F32, name="zs", tag="zs", bufs=3)
-                    for j in range(16):
-                        nc.scalar.activation(
-                            out=pr[:, j, :],
-                            in_=e3[:, j, :],
-                            func=ACT.Exp,
-                            bias=negm[:, j : j + 1],
-                            scale=1.0,
-                            accum_out=z[:, j : j + 1],
-                        )
-                else:
-                    z = work.tile([P, 16], F32, name="zv", tag="zv", bufs=3)
-                    d = work.tile([P, 16, 32], F32, name="d", tag="d", bufs=2)
-                    nc.vector.tensor_tensor(
-                        out=d[:],
-                        in0=e3,
-                        in1=negm[:].unsqueeze(2).to_broadcast([P, 16, 32]),
-                        op=ALU.add,
+        def column_max(k, ct):
+            e3 = st[("e", k, ct)][:].rearrange("p (j i) -> p j i", i=32)
+            negm = work.tile([P, 16], F32, name="negm", tag="negm", bufs=4)
+            nc.vector.tensor_reduce(out=negm[:], in_=e3, axis=AX.X, op=ALU.max, negate=True)
+            st[("negm", k, ct)] = negm
+            if ct == LONG_BANK:
+                d = work.tile([P, 16, 32], F32, name="d", tag="d", bufs=2)
+                nc.vector.tensor_tensor(
+                    out=d[:], in0=e3, in1=negm[:].unsqueeze(2).to_broadcast([P, 16, 32]), op=ALU.add
+                )
+                st[("d", k, ct)] = d
+
+        def exponentials(k, ct):
+            pr = work.tile([P, 16, 32], F32, name="pr", tag="pr", bufs=3)
+            st[("pr", k, ct)] = pr
+            if ct == LONG_BANK:
+                nc.scalar.activation(out=pr[:], in_=st[("d", k, ct)][:], func=ACT.Exp)
+            else:
+                e3 = st[("e", k, ct)][:].rearrange("p (j i) -> p j i", i=32)
+                negm = st[("negm", k, ct)]
+                z = work.tile([P, 16], F32, name="zs", tag="zs", bufs=4)
+                for j in range(16):
+                    nc.scalar.activation(
+                        out=pr[:, j, :],
+                        in_=e3[:, j, :],
+                        func=ACT.Exp,
+                        bias=negm[:, j : j + 1],
+                        scale=1.0,
+                        accum_out=z[:, j : j + 1],
                     )
-                    nc.scalar.activation(out=pr[:], in_=d[:], func=ACT.Exp)
-                    nc.vector.tensor_reduce(out=z[:], in_=pr[:], axis=AX.X, op=ALU.add)
-                rz = work.tile([P, 16], F32, name="rz", tag="rz", bufs=3)
-                nc.vector.reciprocal(out=rz[:], in_=z[:])
-                y = work.tile([P, 16, 32], F32, name="y", tag="y", bufs=3)
-                nc.vector.scalar_tensor_tensor(
-                    out=y[:].rearrange("p j i -> p (j i)"),
-                    in0=e[:],
-                    scalar=bias[:, 4 + ct : 5 + ct],
-                    in1=pr[:].rearrange("p j i -> p (j i)"),
-                    op0=ALU.add,
-                    op1=ALU.mult,
-                )
-                u = work.tile([P, 16, 32], F32, name="u", tag="u", bufs=12)
-                nc.gpsimd.tensor_tensor(
-                    out=u[:],
-                    in0=y[:],
-                    in1=rz[:].unsqueeze(2).to_broadcast([P, 16, 32]),
-                    op=ALU.mult,
-                )
-                u_tiles[(h, ct)] = u
+                st[("z", k, ct)] = z
+
+        def weigh(k, ct):
+            pr = st[("pr", k, ct)]
+            if ct == LONG_BANK:
+                z = work.tile([P, 16], F32, name="zv", tag="zv", bufs=2)
+                nc.vector.tensor_reduce(out=z[:], in_=pr[:], axis=AX.X, op=ALU.add)
+            else:
+                z = st[("z", k, ct)]
+            rz = work.tile([P, 16], F32, name="rz", tag="rz", bufs=6)
+            nc.vector.reciprocal(out=rz[:], in_=z[:])
+            y = work.tile([P, 16, 32], F32, name="y", tag="y", bufs=5)
+            nc.vector.scalar_tensor_tensor(
+                out=y[:].rearrange("p j i -> p (j i)"),
+                in0=st[("e", k, ct)][:],
+                scalar=bias[:, 4 + ct : 5 + ct],
+                in1=pr[:].rearrange("p j i -> p (j i)"),
+                op0=ALU.add,
+                op1=ALU.mult,
+            )
+            u = work.tile([P, 16, 32], F32, name="u", tag="u", bufs=12)
+            nc.gpsimd.tensor_tensor(
+                out=u[:], in0=y[:], in1=rz[:].unsqueeze(2).to_broadcast([P, 16, 32]), op=ALU.mult
+            )
+            st[("u", k, ct)] = u
 
         r_ps = psum.tile([P, 512], F32, name="r_ps", tag="r", bufs=1)
 
-        def batch_end(b):
-            acc = psum.tile([P, 512], F32, name="acc", tag="acc", bufs=1)
-            for ct in range(4):
-                for k in range(8):
-                    h, q = divmod(k, 4)
-                    nc.tensor.matmul(
-                        out=acc[:, 128 * ct : 128 * ct + 128],
-                        lhsT=u_tiles[(h, ct)][:].rearrange("p j i -> p (j i)")[
-                            :, 128 * q : 128 * q + 128
-                        ],
-                        rhs=ident[:],
-                        start=(k == 0),
-                        stop=(k == 7),
-                        is_transpose=True,
-                    )
+        def sum_over_j(b, ct):
+            if ct == 0:
+                acc_new = psum.tile([P, 512], F32, name="acc", tag="tp")
+                st[("acc", b)] = acc_new
+            acc = st[("acc", b)]
+            for n in range(8):
+                h, q = divmod(n, 4)
+                nc.tensor.matmul(
+                    out=acc[:, 128 * ct : 128 * ct + 128],
+                    lhsT=st[("u", 2 * b + h, ct)][:].rearrange("p j i -> p (j i)")[
+                        :, 128 * q : 128 * q + 128
+                    ],
+                    rhs=ident[:],
+                    start=(n == 0),
+                    stop=(n == 7),
+                    is_transpose=True,
+                )
+
+        def fold_copy(b):
             accs = work.tile([P, 512], F32, name="accs", tag="accs")
-            nc.scalar.copy(out=accs[:], in_=acc[:])
+            nc.scalar.copy(out=accs[:], in_=st[("acc", b)][:])
+            st[("accs", b)] = accs
+
+        def fold_mm(b):
             nc.tensor.matmul(
-                out=r_ps[:], lhsT=sel[:, b, :], rhs=accs[:], start=(b == 0), stop=(b == 3)
+                out=r_ps[:], lhsT=sel[:, b, :], rhs=st[("accs", b)][:], start=(b == 0), stop=(b == 3)
             )
 
-        def new_x():
-            prep_weight("go")
+        nxt_sb = const.tile([P, 4, P], F32, name="nxt_sb")
+
+        def new_x_front():
+            quantise_weight("go")
             nxp = psum.tile([P, 4, P], F32, name="nxp", tag="s1")
-            nxt = const.tile([P, 4, P], F32, name="nxt")
             for t in range(4):
                 mx(nxp[:, t, :], "go", t, xc[:], xs[:], True, True)
             for t in range(4):
                 nc.scalar.activation(
-                    out=nxt[:, t, :],
+                    out=nxt_sb[:, t, :],
                     in_=nxp[:, t, :],
                     func=ACT.Tanh,
                     bias=bias[:, 8 + t : 9 + t],
                     scale=1.0,
                 )
-            nxo_ps = psum.tile([P, 512], F32, name="nxo_ps", tag="tp")
+
+        def new_x_back():
+            nxo_ps = psum.tile([P, 512], F32, name="nxo_ps", tag="e", bufs=3)
             for t in range(4):
-                nc.tensor.transpose(nxo_ps[:, 128 * t : 128 * t + 128], nxt[:, t, :], ident[:])
+                nc.tensor.transpose(nxo_ps[:, 128 * t : 128 * t + 128], nxt_sb[:, t, :], ident[:])
             nxo = const.tile([P, 512], F32, name="nxo")
-            nc.scalar.copy(out=nxo[:], in_=nxo_ps[:])
+            nc.vector.tensor_copy(out=nxo[:], in_=nxo_ps[:])
             nc.sync.dma_start(out=out_0.flatten_outer_dims(), in_=nxo[:])
 
-        ops = front(0)
-        for n in range(8):
-            nxt_ops = front(n + 1) if n < 7 else None
-            rel_ops = stage1(n, ops)
-            stage2(n, rel_ops)
-            if n % 2 == 1:
-                batch_end(n // 2)
-            if n == 2:
-                new_x()
-            ops = nxt_ops
+        for m in range(-AHEAD_TRANSPOSE, N_BANKS + BEHIND_FOLD):
+            now = bank_at(m)
+            if now is not None:
+                weigh(now[0], now[1])
+            nxt = bank_at(m + AHEAD_MAX)
+            if nxt is not None:
+                stage2_mm(nxt[0], nxt[1])
+            s1b = bank_at(m + AHEAD_STAGE1)
+            if s1b is not None:
+                stage1_mm(s1b[0], s1b[1])
+            trb = bank_at(m + AHEAD_TRANSPOSE)
+            if trb is not None and trb[1] % 2 == 0:
+                transpose_half(trb[0], trb[1] // 2)
+            b_sum, part = divmod(m - BEHIND_SUM, 8)
+            if 0 <= b_sum < 4 and part in (5, 7):
+                sum_over_j(b_sum, part - 5)
+                sum_over_j(b_sum, part - 4)
+            b_fold, part_fold = divmod(m - BEHIND_FOLD, 8)
+            if 0 <= b_fold < 4 and part_fold == 7:
+                fold_mm(b_fold)
+            exb = bank_at(m + AHEAD_EXP)
+            if exb is not None:
+                exponentials(exb[0], exb[1])
+            if s1b is not None:
+                stage1_tanh(s1b[0], s1b[1])
+            if trb is not None:
+                copy_out(trb[0], trb[1])
+            if 0 <= b_sum < 4 and part == 7:
+                fold_copy(b_sum)
+            if s1b is not None and s1b[1] == 3:
+                regroup_rel(s1b[0])
+                if s1b[0] == 0:
+                    quantise_weight("we")
+                    quantise_rel(0)
+            qrb = bank_at(m + AHEAD_QUANT_REL)
+            if qrb is not None and qrb[1] == 3 and qrb[0] > 0:
+                quantise_rel(qrb[0])
+            qhb = bank_at(m + AHEAD_QUANT_H)
+            if qhb is not None and qhb[1] == 3:
+                quantise_h(qhb[0])
+                spread_xj(qhb[0])
+                if qhb[0] % 2 == 1 and qhb[0] < 7:
+                    spread_xi((qhb[0] + 1) // 2)
+            if nxt is not None:
+                column_max(nxt[0], nxt[1])
+            if m == N_BANKS - 1:
+                new_x_front()
+            if m == N_BANKS + 1:
+                new_x_back()
 
         ro = const.tile([P, 512], F32, name="ro")
         nc.vector.tensor_copy(out=ro[:], in_=r_ps[:])

@@ -42,7 +42,6 @@ def tile_languagemsgencoder_pb_kernel(
         const = ctx.enter_context(tc.tile_pool(name="const", bufs=1))
         work = ctx.enter_context(tc.tile_pool(name="work", bufs=2))
         psum = ctx.enter_context(tc.psum_pool(name="psum", bufs=2))
-        ctx.enter_context(tc.manual_schedule())
 
         braw = const.tile([P, P], BF16, name="braw")
         nc.vector.memset(braw[:], 0.0)

@@ -294,14 +294,16 @@ def tile_languagemsgencoder_pb_kernel(
                     in_=rt[:].rearrange("p t (c i) -> p c t i", i=4),
                 )
             else:
-                nc.gpsimd.tensor_scalar(
-                    out=rg[:],
-                    in0=rt[:].rearrange("p t c -> p c t"),
-                    scalar1=1.0,
-                    scalar2=0.0,
-                    op0=ALU.mult,
-                    op1=ALU.add,
-                )
+                for q in range(4):
+                    cols = slice(128 * q, 128 * q + 128)
+                    nc.gpsimd.tensor_scalar(
+                        out=rg[:, cols, :],
+                        in0=rt[:, :, cols].rearrange("p t c -> p c t"),
+                        scalar1=1.0,
+                        scalar2=0.0,
+                        op0=ALU.mult,
+                        op1=ALU.add,
+                    )
             st[("rg", k)] = rg
 
         def quantise_rel(k):
@@ -316,7 +318,7 @@ def tile_languagemsgencoder_pb_kernel(
 
         def stage2_mm(k, ct):
             rc, rs = st[("r", k)]
-            e = psum.tile([P, 512], F32, name="e", tag="e", bufs=3)
+            e = psum.tile([P, 512], F32, name="e", tag="e", bufs=4)
             mx(e[:], "we", ct, rc[:], rs[:], True, True)
             st[("e", k, ct)] = e
 
@@ -376,7 +378,7 @@ def tile_languagemsgencoder_pb_kernel(
             )
             st[("u", k, ct)] = u
 
-        r_ps = psum.tile([P, 512], F32, name="r_ps", tag="r", bufs=1)
+        ro = const.tile([P, 512], F32, name="ro")
 
         def sum_over_j(b, ct):
             if ct == 0:
@@ -402,9 +404,14 @@ def tile_languagemsgencoder_pb_kernel(
             st[("accs", b)] = accs
 
         def fold_mm(b):
+            fold_ps = psum.tile([P, 512], F32, name="fold_ps", tag="tp")
             nc.tensor.matmul(
-                out=r_ps[:], lhsT=sel[:, b, :], rhs=st[("accs", b)][:], start=(b == 0), stop=(b == 3)
+                out=fold_ps[:], lhsT=sel[:, b, :], rhs=st[("accs", b)][:], start=True, stop=True
             )
+            if b == 0:
+                nc.vector.tensor_copy(out=ro[:], in_=fold_ps[:])
+            else:
+                nc.vector.tensor_tensor(out=ro[:], in0=fold_ps[:], in1=ro[:], op=ALU.add)
 
         nxt_sb = const.tile([P, 4, P], F32, name="nxt_sb")
 
@@ -423,7 +430,7 @@ def tile_languagemsgencoder_pb_kernel(
                 )
 
         def new_x_back():
-            nxo_ps = psum.tile([P, 512], F32, name="nxo_ps", tag="e", bufs=3)
+            nxo_ps = psum.tile([P, 512], F32, name="nxo_ps", tag="e", bufs=4)
             for t in range(4):
                 nc.tensor.transpose(nxo_ps[:, 128 * t : 128 * t + 128], nxt_sb[:, t, :], ident[:])
             nxo = const.tile([P, 512], F32, name="nxo")
@@ -480,6 +487,4 @@ def tile_languagemsgencoder_pb_kernel(
             if m == N_BANKS + 1:
                 new_x_back()
 
-        ro = const.tile([P, 512], F32, name="ro")
-        nc.vector.tensor_copy(out=ro[:], in_=r_ps[:])
         nc.sync.dma_start(out=out_1.flatten_outer_dims(), in_=ro[:])

@@ -17,7 +17,8 @@ P = 128
 FLOPS = 2 * 512 * 512 * (3 * 128 + 2 * 4096)
 
 N_BANKS = 32
-LONG_BANK = 3
+LONG_BANK = 4
+RG_VECTOR_COLS = 256
 AHEAD_MAX = 2
 AHEAD_EXP = 1
 AHEAD_STAGE1 = 8
@@ -288,22 +289,20 @@ def tile_languagemsgencoder_pb_kernel(
         def regroup_rel(k):
             rt = st[("rt", k)]
             rg = work.tile([P, 512, 4], BF16, name="rg", tag="rg", align_bytes=64)
-            if k == 0:
-                nc.vector.tensor_copy(
-                    out=rg[:].rearrange("p (c i) t -> p c t i", i=4),
-                    in_=rt[:].rearrange("p t (c i) -> p c t i", i=4),
+            v_cols = 512 if k == 0 else RG_VECTOR_COLS
+            nc.vector.tensor_copy(
+                out=rg[:, 0:v_cols, :].rearrange("p (c i) t -> p c t i", i=4),
+                in_=rt[:, :, 0:v_cols].rearrange("p t (c i) -> p c t i", i=4),
+            )
+            if v_cols < 512:
+                nc.gpsimd.tensor_scalar(
+                    out=rg[:, v_cols:512, :],
+                    in0=rt[:, :, v_cols:512].rearrange("p t c -> p c t"),
+                    scalar1=1.0,
+                    scalar2=0.0,
+                    op0=ALU.mult,
+                    op1=ALU.add,
                 )
-            else:
-                for q in range(4):
-                    cols = slice(128 * q, 128 * q + 128)
-                    nc.gpsimd.tensor_scalar(
-                        out=rg[:, cols, :],
-                        in0=rt[:, :, cols].rearrange("p t c -> p c t"),
-                        scalar1=1.0,
-                        scalar2=0.0,
-                        op0=ALU.mult,
-                        op1=ALU.add,
-                    )
             st[("rg", k)] = rg
 
         def quantise_rel(k):

@@ -17,7 +17,7 @@ P = 128
 FLOPS = 2 * 512 * 512 * (3 * 128 + 2 * 4096)
 
 N_BANKS = 32
-LONG_BANK = 4
+LONG_BANK = 3
 RG_VECTOR_COLS = 256
 AHEAD_MAX = 2
 AHEAD_EXP = 1

@@ -26,7 +26,6 @@ AHEAD_QUANT_REL = 6
 AHEAD_QUANT_H = 16
 AHEAD_TRANSPOSE = 17
 BEHIND_SUM = 3
-BEHIND_FOLD = 5
 
 
 def bank_at(x):
@@ -66,18 +65,13 @@ def tile_languagemsgencoder_pb_kernel(
                 nc.sync.dma_start(out=w_raw[:], in_=rows.rearrange("(t p) c -> p t c", p=P))
             raw[key] = w_raw
 
-        rel_rows = rel_h.rearrange("b i j k -> b (i j) k")
+        rel_rows = rel_h.rearrange("b i j k -> (b i) j k")
         rel_raw = []
-        for b in range(4):
-            rel_b = const.tile([P, 8, 512], BF16, name="rel_raw%d" % b)
-            rel_raw.append(rel_b)
 
         def load_rel(k):
-            b, h = divmod(k, 2)
-            nc.sync.dma_start(
-                out=rel_raw[b][:, 4 * h : 4 * h + 4, :],
-                in_=rel_rows[b].rearrange("(p g) k -> p g k", g=8)[:, 4 * h : 4 * h + 4, :],
-            )
+            rel_k = const.tile([P, 4, 512], BF16, name="rel_raw%d" % k)
+            nc.sync.dma_start(out=rel_k[:], in_=rel_rows[:, 4 * k : 4 * k + 4, :])
+            rel_raw.append(rel_k)
 
         load_weight("gc", W_gr[1024:1536, :], True)
         load_weight("ga", W_gr[0:512, :], True)
@@ -92,16 +86,6 @@ def tile_languagemsgencoder_pb_kernel(
         make_identity(nc, ident[:])
         bf = const.tile([P, P], F32, name="bf")
         nc.gpsimd.tensor_copy(out=bf[:], in_=braw[:])
-        sel = const.tile([P, 4, P], F32, name="sel")
-        nc.gpsimd.memset(sel[:], 0.0)
-        fold_a = const.tile([P, 32], F32, name="fold_a")
-        fold_b = const.tile([P, 32], F32, name="fold_b")
-        nc.gpsimd.tensor_tensor(out=fold_a[:], in0=ident[:, 0:32], in1=ident[:, 32:64], op=ALU.add)
-        nc.gpsimd.tensor_tensor(out=fold_b[:], in0=ident[:, 64:96], in1=ident[:, 96:128], op=ALU.add)
-        for b in range(4):
-            nc.gpsimd.tensor_tensor(
-                out=sel[:, b, 32 * b : 32 * b + 32], in0=fold_a[:], in1=fold_b[:], op=ALU.add
-            )
 
         xc = const.tile([P, P], U32, name="xc", align_bytes=64)
         xs = const.tile([P, P], U8, name="xs", align_bytes=64)
@@ -133,7 +117,7 @@ def tile_languagemsgencoder_pb_kernel(
         wg = {}
 
         def regroup_weight(key, engine):
-            grouped = const.tile([P, 512, 4], BF16, name="wg_" + key, align_bytes=64)
+            grouped = work.tile([P, 512, 4], BF16, name="wg", tag="wg", bufs=3, align_bytes=64)
             if engine == "g":
                 nc.gpsimd.tensor_scalar(
                     out=grouped[:],
@@ -163,23 +147,6 @@ def tile_languagemsgencoder_pb_kernel(
             wc[key] = codes
             ws[key] = scales
 
-        a_codes = {}
-        a_scales = {}
-
-        def spread_xi(b):
-            ac = const.tile([P, 512], U32, name="ac%d" % b, align_bytes=64)
-            asc = const.tile([P, 512], U8, name="as%d" % b, align_bytes=64)
-            nc.vector.tensor_copy(
-                out=ac[:].bitcast(I32).rearrange("p (r c) -> p r c", r=16),
-                in_=xc[:, 32 * b : 32 * b + 32].bitcast(I32).unsqueeze(1).to_broadcast([P, 16, 32]),
-            )
-            nc.vector.tensor_copy(
-                out=asc[:].bitcast(I32).rearrange("p (r c) -> p r c", r=16),
-                in_=xs[:, 32 * b : 32 * b + 32].bitcast(I32).unsqueeze(1).to_broadcast([P, 16, 8]),
-            )
-            a_codes[b] = ac
-            a_scales[b] = asc
-
         regroup_weight("gc", "v")
         quantise_weight("gc")
         regroup_weight("ga", "s")
@@ -188,7 +155,16 @@ def tile_languagemsgencoder_pb_kernel(
             scales=x4s[:],
             in_=x4[:].rearrange("p c r u -> p (c r u)").bitcast(BF16),
         )
-        spread_xi(0)
+        xi_c = const.tile([P, 512], U32, name="xi_c", align_bytes=64)
+        xi_s = const.tile([P, 512], U8, name="xi_s", align_bytes=64)
+        nc.vector.tensor_copy(
+            out=xi_c[:].bitcast(I32).rearrange("p (r c) -> p r c", r=4),
+            in_=xc[:].bitcast(I32).unsqueeze(1).to_broadcast([P, 4, P]),
+        )
+        nc.vector.tensor_copy(
+            out=xi_s[:].bitcast(I32).rearrange("p (r c) -> p r c", r=4),
+            in_=xs[:].bitcast(I32).unsqueeze(1).to_broadcast([P, 4, 32]),
+        )
         regroup_weight("gb", "v")
         quantise_weight("ga")
         quantise_weight("gb")
@@ -209,28 +185,21 @@ def tile_languagemsgencoder_pb_kernel(
         st = {}
 
         def transpose_half(k, gp):
-            b, h = divmod(k, 2)
-            relw = rel_raw[b][:].rearrange("p g k -> p (g k)").bitcast(F32)
+            relw = rel_raw[k][:].rearrange("p g k -> p (g k)").bitcast(F32)
             tp = psum.tile([P, 2, 2, P], F32, name="tp", tag="tp")
             for q in range(2):
-                g = 4 * h + 2 * gp + q
                 for u in range(2):
-                    lo = 256 * g + 128 * u
+                    lo = 256 * (2 * gp + q) + 128 * u
                     nc.tensor.transpose(tp[:, q, u, :], relw[:, lo : lo + 128], ident[:])
             st[("tp", k, gp)] = tp
 
-        def copy_out(k, gl):
-            if gl == 0:
+        def copy_out(k, gp):
+            if gp == 0:
                 hg_new = work.tile([P, 512, 2], F32, name="hg", tag="hg", align_bytes=64)
                 st[("hg", k)] = hg_new
-            hg = st[("hg", k)]
-            gp, q = divmod(gl, 2)
-            dst = hg[:, 128 * gl : 128 * gl + 128, :].rearrange("p (a i) u -> p a i u", a=4)
-            src = st[("tp", k, gp)][:, q, :, :].rearrange("p u (i a) -> p a i u", a=4)
-            if gp == 0:
-                nc.scalar.copy(out=dst, in_=src)
-            else:
-                nc.vector.tensor_copy(out=dst, in_=src)
+            dst = st[("hg", k)][:, 256 * gp : 256 * gp + 256, :].rearrange("p (q c) u -> p q c u", q=2)
+            src = st[("tp", k, gp)][:].rearrange("p q u c -> p q c u")
+            nc.scalar.copy(out=dst, in_=src)
 
         def quantise_h(k):
             hc = work.tile([P, 512], U32, name="hc", tag="hc", bufs=4, align_bytes=64)
@@ -243,23 +212,21 @@ def tile_languagemsgencoder_pb_kernel(
             st[("h", k)] = (hc, hs)
 
         def spread_xj(k):
-            b, h = divmod(k, 2)
-            bc = work.tile([P, 512], U32, name="bc", tag="bc", bufs=4, align_bytes=64)
-            bs = work.tile([P, 512], U8, name="bs", tag="bs", bufs=4, align_bytes=64)
-            tok = slice(32 * b, 32 * b + 32)
+            bc = work.tile([P, 512], U32, name="bc", tag="bc", bufs=8, align_bytes=64)
+            bs = work.tile([P, 512], U8, name="bs", tag="bs", bufs=8, align_bytes=64)
             nc.vector.tensor_copy(
-                out=bc[:].bitcast(I32).rearrange("p (g a i) -> p g a i", g=4, a=4),
-                in_=xc[:, tok]
+                out=bc[:].bitcast(I32).rearrange("p (j b i) -> p j b i", j=4, b=4),
+                in_=xc[:]
                 .bitcast(I32)
-                .rearrange("p (a h g) -> p h g a", a=4, h=2)[:, h, :, :]
+                .rearrange("p (b j) -> p j b", b=4)[:, 4 * k : 4 * k + 4, :]
                 .unsqueeze(3)
                 .to_broadcast([P, 4, 4, 32]),
             )
             nc.vector.tensor_copy(
-                out=bs[:].bitcast(I32).rearrange("p (g a w) -> p g a w", g=4, a=4),
+                out=bs[:].bitcast(I32).rearrange("p (j b w) -> p j b w", j=4, b=4),
                 in_=x4s[:]
-                .bitcast(I32)[:, tok]
-                .rearrange("p (a h g) -> p h g a", a=4, h=2)[:, h, :, :]
+                .bitcast(I32)
+                .rearrange("p (b j) -> p j b", b=4)[:, 4 * k : 4 * k + 4, :]
                 .unsqueeze(3)
                 .to_broadcast([P, 4, 4, 8]),
             )
@@ -270,7 +237,7 @@ def tile_languagemsgencoder_pb_kernel(
             bc, bs = st[("xj", k)]
             s1 = psum.tile([P, 512], F32, name="s1", tag="s1")
             mx(s1[:], "gc", t, hc[:], hs[:], True, False)
-            mx(s1[:], "ga", t, a_codes[k // 2][:], a_scales[k // 2][:], False, False)
+            mx(s1[:], "ga", t, xi_c[:], xi_s[:], False, False)
             mx(s1[:], "gb", t, bc[:], bs[:], False, True)
             st[("s1", k, t)] = s1
 
@@ -379,17 +346,17 @@ def tile_languagemsgencoder_pb_kernel(
 
         ro = const.tile([P, 512], F32, name="ro")
 
-        def sum_over_j(b, ct):
+        def sum_over_j(pair, ct):
             if ct == 0:
                 acc_new = psum.tile([P, 512], F32, name="acc", tag="tp")
-                st[("acc", b)] = acc_new
-            acc = st[("acc", b)]
+                st[("acc", pair)] = acc_new
+            acc = st[("acc", pair)]
             for n in range(8):
-                h, q = divmod(n, 4)
+                h, jj = divmod(n, 4)
                 nc.tensor.matmul(
                     out=acc[:, 128 * ct : 128 * ct + 128],
-                    lhsT=st[("u", 2 * b + h, ct)][:].rearrange("p j i -> p (j i)")[
-                        :, 128 * q : 128 * q + 128
+                    lhsT=st[("u", 2 * pair + h, ct)][:].rearrange("p j i -> p (j i)")[
+                        :, 128 * jj : 128 * jj + 128
                     ],
                     rhs=ident[:],
                     start=(n == 0),
@@ -397,20 +364,12 @@ def tile_languagemsgencoder_pb_kernel(
                     is_transpose=True,
                 )
 
-        def fold_copy(b):
-            accs = work.tile([P, 512], F32, name="accs", tag="accs")
-            nc.scalar.copy(out=accs[:], in_=st[("acc", b)][:])
-            st[("accs", b)] = accs
-
-        def fold_mm(b):
-            fold_ps = psum.tile([P, 512], F32, name="fold_ps", tag="tp")
-            nc.tensor.matmul(
-                out=fold_ps[:], lhsT=sel[:, b, :], rhs=st[("accs", b)][:], start=True, stop=True
-            )
-            if b == 0:
-                nc.vector.tensor_copy(out=ro[:], in_=fold_ps[:])
+        def add_up(pair):
+            acc = st[("acc", pair)]
+            if pair == 0:
+                nc.vector.tensor_copy(out=ro[:], in_=acc[:])
             else:
-                nc.vector.tensor_tensor(out=ro[:], in0=fold_ps[:], in1=ro[:], op=ALU.add)
+                nc.vector.tensor_tensor(out=ro[:], in0=acc[:], in1=ro[:], op=ALU.add)
 
         nxt_sb = const.tile([P, 4, P], F32, name="nxt_sb")
 
@@ -436,7 +395,7 @@ def tile_languagemsgencoder_pb_kernel(
             nc.vector.tensor_copy(out=nxo[:], in_=nxo_ps[:])
             nc.sync.dma_start(out=out_0.flatten_outer_dims(), in_=nxo[:])
 
-        for m in range(-AHEAD_TRANSPOSE, N_BANKS + BEHIND_FOLD):
+        for m in range(-AHEAD_TRANSPOSE, N_BANKS + BEHIND_SUM):
             now = bank_at(m)
             if now is not None:
                 weigh(now[0], now[1])
@@ -449,22 +408,17 @@ def tile_languagemsgencoder_pb_kernel(
             trb = bank_at(m + AHEAD_TRANSPOSE)
             if trb is not None and trb[1] % 2 == 0:
                 transpose_half(trb[0], trb[1] // 2)
-            b_sum, part = divmod(m - BEHIND_SUM, 8)
-            if 0 <= b_sum < 4 and part in (5, 7):
-                sum_over_j(b_sum, part - 5)
-                sum_over_j(b_sum, part - 4)
-            b_fold, part_fold = divmod(m - BEHIND_FOLD, 8)
-            if 0 <= b_fold < 4 and part_fold == 7:
-                fold_mm(b_fold)
+            pair, part = divmod(m - BEHIND_SUM, 8)
+            if 0 <= pair < 4 and part in (5, 7):
+                sum_over_j(pair, part - 5)
+                sum_over_j(pair, part - 4)
             exb = bank_at(m + AHEAD_EXP)
             if exb is not None:
                 exponentials(exb[0], exb[1])
             if s1b is not None:
                 stage1_tanh(s1b[0], s1b[1])
-            if trb is not None:
-                copy_out(trb[0], trb[1])
-            if 0 <= b_sum < 4 and part == 7:
-                fold_copy(b_sum)
+            if trb is not None and trb[1] % 2 == 0:
+                copy_out(trb[0], trb[1] // 2)
             if s1b is not None and s1b[1] == 3:
                 regroup_rel(s1b[0])
                 if s1b[0] == 0:
@@ -476,9 +430,11 @@ def tile_languagemsgencoder_pb_kernel(
             qhb = bank_at(m + AHEAD_QUANT_H)
             if qhb is not None and qhb[1] == 3:
                 quantise_h(qhb[0])
-                spread_xj(qhb[0])
-                if qhb[0] % 2 == 1 and qhb[0] < 7:
-                    spread_xi((qhb[0] + 1) // 2)
+                if qhb[0] == 0:
+                    for k in range(8):
+                        spread_xj(k)
+            if 0 <= pair < 4 and part == 7:
+                add_up(pair)
             if nxt is not None:
                 column_max(nxt[0], nxt[1])
             if m == N_BANKS - 1:

@@ -199,7 +199,10 @@ def tile_languagemsgencoder_pb_kernel(
                 st[("hg", k)] = hg_new
             dst = st[("hg", k)][:, 256 * gp : 256 * gp + 256, :].rearrange("p (q c) u -> p q c u", q=2)
             src = st[("tp", k, gp)][:].rearrange("p q u c -> p q c u")
-            nc.scalar.copy(out=dst, in_=src)
+            if gp == 1 and k % 2 == 0:
+                nc.vector.tensor_copy(out=dst, in_=src)
+            else:
+                nc.scalar.copy(out=dst, in_=src)
 
         def quantise_h(k):
             hc = work.tile([P, 512], U32, name="hc", tag="hc", bufs=4, align_bytes=64)

@@ -342,9 +342,13 @@ def tile_languagemsgencoder_pb_kernel(
                 op1=ALU.mult,
             )
             u = work.tile([P, 16, 32], F32, name="u", tag="u", bufs=12)
-            nc.gpsimd.tensor_tensor(
-                out=u[:], in0=y[:], in1=rz[:].unsqueeze(2).to_broadcast([P, 16, 32]), op=ALU.mult
-            )
+            for h in range(2):
+                nc.gpsimd.tensor_tensor(
+                    out=u[:, 8 * h : 8 * h + 8, :],
+                    in0=y[:, 8 * h : 8 * h + 8, :],
+                    in1=rz[:, 8 * h : 8 * h + 8].unsqueeze(2).to_broadcast([P, 8, 32]),
+                    op=ALU.mult,
+                )
             st[("u", k, ct)] = u
 
         ro = const.tile([P, 512], F32, name="ro")

@@ -17,15 +17,18 @@ P = 128
 FLOPS = 2 * 512 * 512 * (3 * 128 + 2 * 4096)
 
 N_BANKS = 32
-LONG_BANK = 3
-RG_VECTOR_COLS = 256
-AHEAD_MAX = 2
+SHORT = 12
 AHEAD_EXP = 1
-AHEAD_STAGE1 = 8
-AHEAD_QUANT_REL = 6
-AHEAD_QUANT_H = 16
-AHEAD_TRANSPOSE = 17
-BEHIND_SUM = 3
+AHEAD_MAX = 2
+AHEAD_STAGE2 = 3
+AHEAD_QUANT_REL = 4
+AHEAD_REGROUP = 5
+AHEAD_TANH = 9
+AHEAD_STAGE1 = 10
+AHEAD_SPREAD = 12
+AHEAD_QUANT_H = 14
+AHEAD_TRANSPOSE = 18
+BEHIND_SUM = 11
 
 
 def bank_at(x):
@@ -84,33 +87,29 @@ def tile_languagemsgencoder_pb_kernel(
 
         ident = const.tile([P, P], F32, name="ident")
         make_identity(nc, ident[:])
-        bf = const.tile([P, P], F32, name="bf")
-        nc.gpsimd.tensor_copy(out=bf[:], in_=braw[:])
 
         xc = const.tile([P, P], U32, name="xc", align_bytes=64)
         xs = const.tile([P, P], U8, name="xs", align_bytes=64)
-        x4c = const.tile([P, 512], U32, name="x4c", align_bytes=64)
         x4s = const.tile([P, 512], U8, name="x4s", align_bytes=64)
         nc.vector.memset(xs[:].bitcast(I32), 0)
         nc.vector.memset(x4s[:].bitcast(I32), 0)
 
+        ctx.enter_context(
+            tc.manual_schedule(
+                engines={
+                    mybir.EngineType.PE,
+                    mybir.EngineType.Activation,
+                    mybir.EngineType.DVE,
+                    mybir.EngineType.Pool,
+                }
+            )
+        )
         xw = x_sb[:].bitcast(F32)
         xt = psum.tile([P, 2, 2, P], F32, name="xt", tag="tp")
         for u in range(2):
             nc.tensor.transpose(xt[:, 0, u, :], xw[:, 128 * u : 128 * u + 128], ident[:])
-        bt = psum.tile([P, 512], F32, name="bt", tag="tp")
-        nc.tensor.transpose(bt[:, 0:P], bf[:], ident[:])
         xg = const.tile([P, P, 2], F32, name="xg", align_bytes=64)
-        nc.vector.tensor_copy(out=xg[:], in_=xt[:, 0, :, :].rearrange("p u c -> p c u"))
-        x4 = const.tile([P, P, 4, 2], F32, name="x4", align_bytes=64)
-        nc.scalar.copy(out=x4[:], in_=xg[:].unsqueeze(2).to_broadcast([P, P, 4, 2]))
-        bias = const.tile([P, 12], F32, name="bias")
-        nc.scalar.copy(out=bias[:], in_=bt[:, 0:12])
-        nc.vector.quantize_mx(
-            out=xc[:].bitcast(FP8X4),
-            scales=xs[:],
-            in_=xg[:].rearrange("p c u -> p (c u)").bitcast(BF16),
-        )
+        nc.scalar.copy(out=xg[:], in_=xt[:, 0, :, :].rearrange("p u c -> p c u"))
 
         wc = {}
         ws = {}
@@ -119,14 +118,15 @@ def tile_languagemsgencoder_pb_kernel(
         def regroup_weight(key, engine):
             grouped = work.tile([P, 512, 4], BF16, name="wg", tag="wg", bufs=3, align_bytes=64)
             if engine == "g":
-                nc.gpsimd.tensor_scalar(
-                    out=grouped[:],
-                    in0=raw[key][:].rearrange("p t c -> p c t"),
-                    scalar1=1.0,
-                    scalar2=0.0,
-                    op0=ALU.mult,
-                    op1=ALU.add,
-                )
+                for h in range(4):
+                    nc.gpsimd.tensor_scalar(
+                        out=grouped[:, 128 * h : 128 * h + 128, :],
+                        in0=raw[key][:, :, 128 * h : 128 * h + 128].rearrange("p t c -> p c t"),
+                        scalar1=1.0,
+                        scalar2=0.0,
+                        op0=ALU.mult,
+                        op1=ALU.add,
+                    )
             else:
                 dst = grouped[:].rearrange("p (c i) t -> p c t i", i=4)
                 src = raw[key][:].rearrange("p t (c i) -> p c t i", i=4)
@@ -148,28 +148,17 @@ def tile_languagemsgencoder_pb_kernel(
             ws[key] = scales
 
         regroup_weight("gc", "v")
+        nc.vector.quantize_mx(
+            out=xc[:].bitcast(FP8X4),
+            scales=xs[:],
+            in_=xg[:].rearrange("p c u -> p (c u)").bitcast(BF16),
+        )
         quantise_weight("gc")
         regroup_weight("ga", "s")
-        nc.vector.quantize_mx(
-            out=x4c[:].bitcast(FP8X4),
-            scales=x4s[:],
-            in_=x4[:].rearrange("p c r u -> p (c r u)").bitcast(BF16),
-        )
-        xi_c = const.tile([P, 512], U32, name="xi_c", align_bytes=64)
-        xi_s = const.tile([P, 512], U8, name="xi_s", align_bytes=64)
-        nc.vector.tensor_copy(
-            out=xi_c[:].bitcast(I32).rearrange("p (r c) -> p r c", r=4),
-            in_=xc[:].bitcast(I32).unsqueeze(1).to_broadcast([P, 4, P]),
-        )
-        nc.vector.tensor_copy(
-            out=xi_s[:].bitcast(I32).rearrange("p (r c) -> p r c", r=4),
-            in_=xs[:].bitcast(I32).unsqueeze(1).to_broadcast([P, 4, 32]),
-        )
-        regroup_weight("gb", "v")
-        quantise_weight("ga")
-        quantise_weight("gb")
-        regroup_weight("we", "g")
-        regroup_weight("go", "g")
+        for r in range(4):
+            nc.gpsimd.tensor_copy(out=x4s[:].rearrange("p (c r) -> p c r", r=4)[:, :, r], in_=xs[:])
+        bf = const.tile([P, P], F32, name="bf")
+        nc.gpsimd.tensor_copy(out=bf[:], in_=braw[:])
 
         def mx(out, key, t, rhs, rhs_scale, start, stop):
             nc.tensor.matmul_mx(
@@ -199,7 +188,7 @@ def tile_languagemsgencoder_pb_kernel(
                 st[("hg", k)] = hg_new
             dst = st[("hg", k)][:, 256 * gp : 256 * gp + 256, :].rearrange("p (q c) u -> p q c u", q=2)
             src = st[("tp", k, gp)][:].rearrange("p q u c -> p q c u")
-            if gp == 1 and k % 2 == 0:
+            if k == 0 and gp == 0:
                 nc.vector.tensor_copy(out=dst, in_=src)
             else:
                 nc.scalar.copy(out=dst, in_=src)
@@ -214,34 +203,36 @@ def tile_languagemsgencoder_pb_kernel(
             )
             st[("h", k)] = (hc, hs)
 
-        def spread_xj(k):
-            bc = work.tile([P, 512], U32, name="bc", tag="bc", bufs=8, align_bytes=64)
-            bs = work.tile([P, 512], U8, name="bs", tag="bs", bufs=8, align_bytes=64)
+        bc = const.tile([P, 8 * 512], U32, name="bc", align_bytes=64)
+        bs = const.tile([P, 8 * 512], U8, name="bs", align_bytes=64)
+
+        def spread_xj(k0, k1):
+            j0, nj = 4 * k0, 4 * (k1 - k0)
             nc.vector.tensor_copy(
-                out=bc[:].bitcast(I32).rearrange("p (j b i) -> p j b i", j=4, b=4),
+                out=bc[:, 512 * k0 : 512 * k1].bitcast(I32).rearrange("p (j b i) -> p j b i", j=nj, b=4),
                 in_=xc[:]
                 .bitcast(I32)
-                .rearrange("p (b j) -> p j b", b=4)[:, 4 * k : 4 * k + 4, :]
+                .rearrange("p (b j) -> p j b", b=4)[:, j0 : j0 + nj, :]
                 .unsqueeze(3)
-                .to_broadcast([P, 4, 4, 32]),
+                .to_broadcast([P, nj, 4, 32]),
             )
             nc.vector.tensor_copy(
-                out=bs[:].bitcast(I32).rearrange("p (j b w) -> p j b w", j=4, b=4),
+                out=bs[:, 512 * k0 : 512 * k1].bitcast(I32).rearrange("p (j b w) -> p j b w", j=nj, b=4),
                 in_=x4s[:]
                 .bitcast(I32)
-                .rearrange("p (b j) -> p j b", b=4)[:, 4 * k : 4 * k + 4, :]
+                .rearrange("p (b j) -> p j b", b=4)[:, j0 : j0 + nj, :]
                 .unsqueeze(3)
-                .to_broadcast([P, 4, 4, 8]),
+                .to_broadcast([P, nj, 4, 8]),
             )
-            st[("xj", k)] = (bc, bs)
+
+        bias = const.tile([P, 12], F32, name="bias")
 
         def stage1_mm(k, t):
             hc, hs = st[("h", k)]
-            bc, bs = st[("xj", k)]
             s1 = psum.tile([P, 512], F32, name="s1", tag="s1")
             mx(s1[:], "gc", t, hc[:], hs[:], True, False)
             mx(s1[:], "ga", t, xi_c[:], xi_s[:], False, False)
-            mx(s1[:], "gb", t, bc[:], bs[:], False, True)
+            mx(s1[:], "gb", t, bc[:, 512 * k : 512 * k + 512], bs[:, 512 * k : 512 * k + 512], False, True)
             st[("s1", k, t)] = s1
 
         def stage1_tanh(k, t):
@@ -259,20 +250,10 @@ def tile_languagemsgencoder_pb_kernel(
         def regroup_rel(k):
             rt = st[("rt", k)]
             rg = work.tile([P, 512, 4], BF16, name="rg", tag="rg", align_bytes=64)
-            v_cols = 512 if k == 0 else RG_VECTOR_COLS
             nc.vector.tensor_copy(
-                out=rg[:, 0:v_cols, :].rearrange("p (c i) t -> p c t i", i=4),
-                in_=rt[:, :, 0:v_cols].rearrange("p t (c i) -> p c t i", i=4),
+                out=rg[:].rearrange("p (c i) t -> p c t i", i=4),
+                in_=rt[:].rearrange("p t (c i) -> p c t i", i=4),
             )
-            if v_cols < 512:
-                nc.gpsimd.tensor_scalar(
-                    out=rg[:, v_cols:512, :],
-                    in0=rt[:, :, v_cols:512].rearrange("p t c -> p c t"),
-                    scalar1=1.0,
-                    scalar2=0.0,
-                    op0=ALU.mult,
-                    op1=ALU.add,
-                )
             st[("rg", k)] = rg
 
         def quantise_rel(k):
@@ -296,59 +277,70 @@ def tile_languagemsgencoder_pb_kernel(
             negm = work.tile([P, 16], F32, name="negm", tag="negm", bufs=4)
             nc.vector.tensor_reduce(out=negm[:], in_=e3, axis=AX.X, op=ALU.max, negate=True)
             st[("negm", k, ct)] = negm
-            if ct == LONG_BANK:
-                d = work.tile([P, 16, 32], F32, name="d", tag="d", bufs=2)
-                nc.vector.tensor_tensor(
-                    out=d[:], in0=e3, in1=negm[:].unsqueeze(2).to_broadcast([P, 16, 32]), op=ALU.add
-                )
-                st[("d", k, ct)] = d
 
-        def exponentials(k, ct):
+        def subtract_max(k, ct):
+            e3 = st[("e", k, ct)][:].rearrange("p (j i) -> p j i", i=32)
+            d = work.tile([P, 16 - SHORT, 32], F32, name="d", tag="d", bufs=3)
+            nc.vector.tensor_tensor(
+                out=d[:],
+                in0=e3[:, SHORT:16, :],
+                in1=st[("negm", k, ct)][:, SHORT:16].unsqueeze(2).to_broadcast([P, 16 - SHORT, 32]),
+                op=ALU.add,
+            )
+            st[("d", k, ct)] = d
+
+        def short_exponentials(k, ct):
             pr = work.tile([P, 16, 32], F32, name="pr", tag="pr", bufs=3)
             st[("pr", k, ct)] = pr
-            if ct == LONG_BANK:
-                nc.scalar.activation(out=pr[:], in_=st[("d", k, ct)][:], func=ACT.Exp)
-            else:
-                e3 = st[("e", k, ct)][:].rearrange("p (j i) -> p j i", i=32)
-                negm = st[("negm", k, ct)]
-                z = work.tile([P, 16], F32, name="zs", tag="zs", bufs=4)
-                for j in range(16):
-                    nc.scalar.activation(
-                        out=pr[:, j, :],
-                        in_=e3[:, j, :],
-                        func=ACT.Exp,
-                        bias=negm[:, j : j + 1],
-                        scale=1.0,
-                        accum_out=z[:, j : j + 1],
-                    )
-                st[("z", k, ct)] = z
+            e3 = st[("e", k, ct)][:].rearrange("p (j i) -> p j i", i=32)
+            negm = st[("negm", k, ct)]
+            z = work.tile([P, 16], F32, name="zs", tag="zs", bufs=4)
+            for j in range(SHORT):
+                nc.scalar.activation(
+                    out=pr[:, j, :],
+                    in_=e3[:, j, :],
+                    func=ACT.Exp,
+                    bias=negm[:, j : j + 1],
+                    scale=1.0,
+                    accum_out=z[:, j : j + 1],
+                )
+            st[("z", k, ct)] = z
+
+        def long_exponential(k, ct):
+            nc.scalar.activation(
+                out=st[("pr", k, ct)][:, SHORT:16, :], in_=st[("d", k, ct)][:], func=ACT.Exp
+            )
+
+        def sum_exponentials(k, ct):
+            nc.vector.tensor_reduce(
+                out=st[("z", k, ct)][:, SHORT:16],
+                in_=st[("pr", k, ct)][:, SHORT:16, :],
+                axis=AX.X,
+                op=ALU.add,
+            )
 
         def weigh(k, ct):
-            pr = st[("pr", k, ct)]
-            if ct == LONG_BANK:
-                z = work.tile([P, 16], F32, name="zv", tag="zv", bufs=2)
-                nc.vector.tensor_reduce(out=z[:], in_=pr[:], axis=AX.X, op=ALU.add)
-            else:
-                z = st[("z", k, ct)]
-            rz = work.tile([P, 16], F32, name="rz", tag="rz", bufs=6)
-            nc.vector.reciprocal(out=rz[:], in_=z[:])
             y = work.tile([P, 16, 32], F32, name="y", tag="y", bufs=5)
             nc.vector.scalar_tensor_tensor(
                 out=y[:].rearrange("p j i -> p (j i)"),
                 in0=st[("e", k, ct)][:],
                 scalar=bias[:, 4 + ct : 5 + ct],
-                in1=pr[:].rearrange("p j i -> p (j i)"),
+                in1=st[("pr", k, ct)][:].rearrange("p j i -> p (j i)"),
                 op0=ALU.add,
                 op1=ALU.mult,
             )
-            u = work.tile([P, 16, 32], F32, name="u", tag="u", bufs=12)
-            for h in range(2):
-                nc.gpsimd.tensor_tensor(
-                    out=u[:, 8 * h : 8 * h + 8, :],
-                    in0=y[:, 8 * h : 8 * h + 8, :],
-                    in1=rz[:, 8 * h : 8 * h + 8].unsqueeze(2).to_broadcast([P, 8, 32]),
-                    op=ALU.mult,
-                )
+            st[("y", k, ct)] = y
+
+        def normalise(k, ct, engine):
+            rz = work.tile([P, 16], F32, name="rz", tag="rz", bufs=4)
+            nc.vector.reciprocal(out=rz[:], in_=st[("z", k, ct)][:])
+            u = work.tile([P, 16, 32], F32, name="u", tag="u", bufs=16)
+            engine.tensor_tensor(
+                out=u[:],
+                in0=st[("y", k, ct)][:],
+                in1=rz[:].unsqueeze(2).to_broadcast([P, 16, 32]),
+                op=ALU.mult,
+            )
             st[("u", k, ct)] = u
 
         ro = const.tile([P, 512], F32, name="ro")
@@ -371,17 +363,16 @@ def tile_languagemsgencoder_pb_kernel(
                     is_transpose=True,
                 )
 
-        def add_up(pair):
+        def add_up(pair, lo, hi):
             acc = st[("acc", pair)]
             if pair == 0:
-                nc.vector.tensor_copy(out=ro[:], in_=acc[:])
+                nc.vector.tensor_copy(out=ro[:, lo:hi], in_=acc[:, lo:hi])
             else:
-                nc.vector.tensor_tensor(out=ro[:], in0=acc[:], in1=ro[:], op=ALU.add)
+                nc.vector.tensor_tensor(out=ro[:, lo:hi], in0=acc[:, lo:hi], in1=ro[:, lo:hi], op=ALU.add)
 
         nxt_sb = const.tile([P, 4, P], F32, name="nxt_sb")
 
         def new_x_front():
-            quantise_weight("go")
             nxp = psum.tile([P, 4, P], F32, name="nxp", tag="s1")
             for t in range(4):
                 mx(nxp[:, t, :], "go", t, xc[:], xs[:], True, True)
@@ -399,54 +390,103 @@ def tile_languagemsgencoder_pb_kernel(
             for t in range(4):
                 nc.tensor.transpose(nxo_ps[:, 128 * t : 128 * t + 128], nxt_sb[:, t, :], ident[:])
             nxo = const.tile([P, 512], F32, name="nxo")
-            nc.vector.tensor_copy(out=nxo[:], in_=nxo_ps[:])
+            nc.scalar.copy(out=nxo[:], in_=nxo_ps[:])
             nc.sync.dma_start(out=out_0.flatten_outer_dims(), in_=nxo[:])
 
-        for m in range(-AHEAD_TRANSPOSE, N_BANKS + BEHIND_SUM):
-            now = bank_at(m)
-            if now is not None:
-                weigh(now[0], now[1])
-            nxt = bank_at(m + AHEAD_MAX)
-            if nxt is not None:
-                stage2_mm(nxt[0], nxt[1])
-            s1b = bank_at(m + AHEAD_STAGE1)
-            if s1b is not None:
-                stage1_mm(s1b[0], s1b[1])
-            trb = bank_at(m + AHEAD_TRANSPOSE)
-            if trb is not None and trb[1] % 2 == 0:
-                transpose_half(trb[0], trb[1] // 2)
-            pair, part = divmod(m - BEHIND_SUM, 8)
-            if 0 <= pair < 4 and part in (5, 7):
-                sum_over_j(pair, part - 5)
-                sum_over_j(pair, part - 4)
-            exb = bank_at(m + AHEAD_EXP)
-            if exb is not None:
-                exponentials(exb[0], exb[1])
-            if s1b is not None:
-                stage1_tanh(s1b[0], s1b[1])
-            if trb is not None and trb[1] % 2 == 0:
-                copy_out(trb[0], trb[1] // 2)
-            if s1b is not None and s1b[1] == 3:
-                regroup_rel(s1b[0])
-                if s1b[0] == 0:
-                    quantise_weight("we")
-                    quantise_rel(0)
-            qrb = bank_at(m + AHEAD_QUANT_REL)
-            if qrb is not None and qrb[1] == 3 and qrb[0] > 0:
-                quantise_rel(qrb[0])
-            qhb = bank_at(m + AHEAD_QUANT_H)
-            if qhb is not None and qhb[1] == 3:
-                quantise_h(qhb[0])
-                if qhb[0] == 0:
-                    for k in range(8):
-                        spread_xj(k)
-            if 0 <= pair < 4 and part == 7:
-                add_up(pair)
-            if nxt is not None:
-                column_max(nxt[0], nxt[1])
-            if m == N_BANKS - 1:
-                new_x_front()
-            if m == N_BANKS + 1:
-                new_x_back()
+        for gp in range(2):
+            transpose_half(0, gp)
+            copy_out(0, gp)
+        quantise_weight("ga")
+        regroup_weight("gb", "v")
+        quantise_h(0)
+        quantise_weight("gb")
+        regroup_weight("we", "s")
+        xi_c = const.tile([P, 512], U32, name="xi_c", align_bytes=64)
+        xi_s = const.tile([P, 512], U8, name="xi_s", align_bytes=64)
+        nc.vector.tensor_copy(
+            out=xi_c[:].bitcast(I32).rearrange("p (r c) -> p r c", r=4),
+            in_=xc[:].bitcast(I32).unsqueeze(1).to_broadcast([P, 4, P]),
+        )
+        nc.vector.tensor_copy(
+            out=xi_s[:].bitcast(I32).rearrange("p (r c) -> p r c", r=4),
+            in_=xs[:].bitcast(I32).unsqueeze(1).to_broadcast([P, 4, 32]),
+        )
+        spread_xj(0, 1)
+        bt = psum.tile([P, 512], F32, name="bt", tag="tp")
+        nc.tensor.transpose(bt[:, 0:P], bf[:], ident[:])
+        nc.scalar.copy(out=bias[:], in_=bt[:, 0:12])
+        quantise_weight("we")
+        regroup_weight("go", "g")
 
-        nc.sync.dma_start(out=out_1.flatten_outer_dims(), in_=ro[:])
+        def unit_at(s, ahead, first):
+            k, part = divmod(s + ahead, 4)
+            return k if part == 0 and first <= k < 8 else None
+
+        for s in range(-AHEAD_TRANSPOSE, N_BANKS + 2):
+            b = bank_at(s + AHEAD_STAGE2)
+            if b is not None:
+                stage2_mm(b[0], b[1])
+            b = bank_at(s + AHEAD_STAGE1)
+            if b is not None:
+                stage1_mm(b[0], b[1])
+            for gp in range(2):
+                k = unit_at(s, AHEAD_TRANSPOSE - 2 * gp, 1)
+                if k is not None:
+                    transpose_half(k, gp)
+            last = s >= N_BANKS
+            pair, part = (3, s - N_BANKS) if last else divmod(s - BEHIND_SUM, 8)
+            summing = 0 <= pair < (4 if last else 3) and part < 2
+            if summing:
+                sum_over_j(pair, 2 * part)
+                sum_over_j(pair, 2 * part + 1)
+            b = bank_at(s + AHEAD_EXP)
+            if b is not None:
+                short_exponentials(b[0], b[1])
+            b = bank_at(s + AHEAD_TANH)
+            if b is not None:
+                stage1_tanh(b[0], b[1])
+            b = bank_at(s + AHEAD_MAX)
+            if b is not None:
+                column_max(b[0], b[1])
+            b = bank_at(s + AHEAD_EXP)
+            if b is not None:
+                subtract_max(b[0], b[1])
+            now = bank_at(s)
+            if now is not None:
+                sum_exponentials(now[0], now[1])
+                weigh(now[0], now[1])
+            k = unit_at(s, AHEAD_QUANT_REL, 0)
+            if k is not None:
+                quantise_rel(k)
+            k = unit_at(s, AHEAD_QUANT_H, 1)
+            if k is not None:
+                quantise_h(k)
+            k = unit_at(s, AHEAD_SPREAD, 1)
+            if k is not None:
+                spread_xj(k, k + 1)
+            if last:
+                add_up(3, 256 * part, 256 * part + 256)
+                nc.sync.dma_start(
+                    out=out_1.flatten_outer_dims()[:, 256 * part : 256 * part + 256],
+                    in_=ro[:, 256 * part : 256 * part + 256],
+                )
+            elif 0 <= pair < 3 and part == 2:
+                add_up(pair, 0, 512)
+            k = unit_at(s, AHEAD_REGROUP, 0)
+            if k is not None:
+                regroup_rel(k)
+            if s == N_BANKS - 2:
+                quantise_weight("go")
+            if now is not None:
+                normalise(now[0], now[1], nc.vector if s == N_BANKS - 1 else nc.gpsimd)
+            b = bank_at(s + AHEAD_EXP)
+            if b is not None:
+                long_exponential(b[0], b[1])
+            for gp in range(2):
+                k = unit_at(s, AHEAD_TRANSPOSE - 1 - 2 * gp, 1)
+                if k is not None:
+                    copy_out(k, gp)
+            if s == N_BANKS - 1:
+                new_x_front()
+            if s == N_BANKS:
+                new_x_back()

@@ -17,7 +17,7 @@ P = 128
 FLOPS = 2 * 512 * 512 * (3 * 128 + 2 * 4096)
 
 N_BANKS = 32
-SHORT = 12
+LONG_BANK = 3
 AHEAD_EXP = 1
 AHEAD_MAX = 2
 AHEAD_STAGE2 = 3
@@ -25,7 +25,7 @@ AHEAD_QUANT_REL = 4
 AHEAD_REGROUP = 5
 AHEAD_TANH = 9
 AHEAD_STAGE1 = 10
-AHEAD_SPREAD = 12
+AHEAD_SPREAD = 8
 AHEAD_QUANT_H = 14
 AHEAD_TRANSPOSE = 18
 BEHIND_SUM = 11
@@ -188,7 +188,7 @@ def tile_languagemsgencoder_pb_kernel(
                 st[("hg", k)] = hg_new
             dst = st[("hg", k)][:, 256 * gp : 256 * gp + 256, :].rearrange("p (q c) u -> p q c u", q=2)
             src = st[("tp", k, gp)][:].rearrange("p q u c -> p q c u")
-            if k == 0 and gp == 0:
+            if gp == (0 if k == 0 else 1) and k % 2 == 0:
                 nc.vector.tensor_copy(out=dst, in_=src)
             else:
                 nc.scalar.copy(out=dst, in_=src)
@@ -280,22 +280,22 @@ def tile_languagemsgencoder_pb_kernel(
 
         def subtract_max(k, ct):
             e3 = st[("e", k, ct)][:].rearrange("p (j i) -> p j i", i=32)
-            d = work.tile([P, 16 - SHORT, 32], F32, name="d", tag="d", bufs=3)
+            d = work.tile([P, 16, 32], F32, name="d", tag="d", bufs=2)
             nc.vector.tensor_tensor(
                 out=d[:],
-                in0=e3[:, SHORT:16, :],
-                in1=st[("negm", k, ct)][:, SHORT:16].unsqueeze(2).to_broadcast([P, 16 - SHORT, 32]),
+                in0=e3,
+                in1=st[("negm", k, ct)][:].unsqueeze(2).to_broadcast([P, 16, 32]),
                 op=ALU.add,
             )
             st[("d", k, ct)] = d
 
         def short_exponentials(k, ct):
-            pr = work.tile([P, 16, 32], F32, name="pr", tag="pr", bufs=3)
+            pr = work.tile([P, 16, 32], F32, name="pr", tag="pr", bufs=4)
             st[("pr", k, ct)] = pr
             e3 = st[("e", k, ct)][:].rearrange("p (j i) -> p j i", i=32)
             negm = st[("negm", k, ct)]
             z = work.tile([P, 16], F32, name="zs", tag="zs", bufs=4)
-            for j in range(SHORT):
+            for j in range(16):
                 nc.scalar.activation(
                     out=pr[:, j, :],
                     in_=e3[:, j, :],
@@ -307,17 +307,14 @@ def tile_languagemsgencoder_pb_kernel(
             st[("z", k, ct)] = z
 
         def long_exponential(k, ct):
-            nc.scalar.activation(
-                out=st[("pr", k, ct)][:, SHORT:16, :], in_=st[("d", k, ct)][:], func=ACT.Exp
-            )
+            pr = work.tile([P, 16, 32], F32, name="pr", tag="pr", bufs=4)
+            st[("pr", k, ct)] = pr
+            nc.scalar.activation(out=pr[:], in_=st[("d", k, ct)][:], func=ACT.Exp)
 
         def sum_exponentials(k, ct):
-            nc.vector.tensor_reduce(
-                out=st[("z", k, ct)][:, SHORT:16],
-                in_=st[("pr", k, ct)][:, SHORT:16, :],
-                axis=AX.X,
-                op=ALU.add,
-            )
+            z = work.tile([P, 16], F32, name="zv", tag="zv", bufs=2)
+            nc.vector.tensor_reduce(out=z[:], in_=st[("pr", k, ct)][:], axis=AX.X, op=ALU.add)
+            st[("z", k, ct)] = z
 
         def weigh(k, ct):
             y = work.tile([P, 16, 32], F32, name="y", tag="y", bufs=5)
@@ -440,7 +437,7 @@ def tile_languagemsgencoder_pb_kernel(
                 sum_over_j(pair, 2 * part)
                 sum_over_j(pair, 2 * part + 1)
             b = bank_at(s + AHEAD_EXP)
-            if b is not None:
+            if b is not None and b[1] != LONG_BANK:
                 short_exponentials(b[0], b[1])
             b = bank_at(s + AHEAD_TANH)
             if b is not None:
@@ -449,11 +446,12 @@ def tile_languagemsgencoder_pb_kernel(
             if b is not None:
                 column_max(b[0], b[1])
             b = bank_at(s + AHEAD_EXP)
-            if b is not None:
+            if b is not None and b[1] == LONG_BANK:
                 subtract_max(b[0], b[1])
             now = bank_at(s)
             if now is not None:
-                sum_exponentials(now[0], now[1])
+                if now[1] == LONG_BANK:
+                    sum_exponentials(now[0], now[1])
                 weigh(now[0], now[1])
             k = unit_at(s, AHEAD_QUANT_REL, 0)
             if k is not None:
@@ -461,9 +459,8 @@ def tile_languagemsgencoder_pb_kernel(
             k = unit_at(s, AHEAD_QUANT_H, 1)
             if k is not None:
                 quantise_h(k)
-            k = unit_at(s, AHEAD_SPREAD, 1)
-            if k is not None:
-                spread_xj(k, k + 1)
+            if s == -AHEAD_SPREAD:
+                spread_xj(1, 8)
             if last:
                 add_up(3, 256 * part, 256 * part + 256)
                 nc.sync.dma_start(
@@ -480,7 +477,7 @@ def tile_languagemsgencoder_pb_kernel(
             if now is not None:
                 normalise(now[0], now[1], nc.vector if s == N_BANKS - 1 else nc.gpsimd)
             b = bank_at(s + AHEAD_EXP)
-            if b is not None:
+            if b is not None and b[1] == LONG_BANK:
                 long_exponential(b[0], b[1])
             for gp in range(2):
                 k = unit_at(s, AHEAD_TRANSPOSE - 1 - 2 * gp, 1)

@@ -17,7 +17,7 @@ P = 128
 FLOPS = 2 * 512 * 512 * (3 * 128 + 2 * 4096)
 
 N_BANKS = 32
-LONG_BANK = 3
+LONG_BANK = 0
 AHEAD_EXP = 1
 AHEAD_MAX = 2
 AHEAD_STAGE2 = 3
@@ -26,8 +26,8 @@ AHEAD_REGROUP = 5
 AHEAD_TANH = 9
 AHEAD_STAGE1 = 10
 AHEAD_SPREAD = 8
-AHEAD_QUANT_H = 14
-AHEAD_TRANSPOSE = 18
+AHEAD_QUANT_H = 13
+AHEAD_TRANSPOSE = 17
 BEHIND_SUM = 11
 
 
@@ -183,25 +183,30 @@ def tile_languagemsgencoder_pb_kernel(
             st[("tp", k, gp)] = tp
 
         def copy_out(k, gp):
-            if gp == 0:
-                hg_new = work.tile([P, 512, 2], F32, name="hg", tag="hg", align_bytes=64)
-                st[("hg", k)] = hg_new
-            dst = st[("hg", k)][:, 256 * gp : 256 * gp + 256, :].rearrange("p (q c) u -> p q c u", q=2)
+            if k < 2:
+                if gp == 0:
+                    hg_new = work.tile([P, 2048], BF16, name="hg", tag="hg", align_bytes=64)
+                    st[("hg", k)] = hg_new[:]
+            elif gp == 0:
+                hr_new = work.tile([P, 4096], BF16, name="hr", tag="hr", bufs=3, align_bytes=64)
+                st[("hr", k - 2)] = hr_new
+                st[("hg", k)] = hr_new[:, 0:2048]
+            dst = (
+                st[("hg", k)][:, 1024 * gp : 1024 * gp + 1024]
+                .bitcast(F32)
+                .rearrange("p (q c u) -> p q c u", q=2, u=2)
+            )
             src = st[("tp", k, gp)][:].rearrange("p q u c -> p q c u")
-            if gp == (0 if k == 0 else 1) and k % 2 == 0:
+            if gp == 0 and k % 2 == 0:
                 nc.vector.tensor_copy(out=dst, in_=src)
             else:
                 nc.scalar.copy(out=dst, in_=src)
 
         def quantise_h(k):
-            hc = work.tile([P, 512], U32, name="hc", tag="hc", bufs=4, align_bytes=64)
-            hs = work.tile([P, 512], U8, name="hs", tag="hs", bufs=4, align_bytes=64)
-            nc.vector.quantize_mx(
-                out=hc[:].bitcast(FP8X4),
-                scales=hs[:],
-                in_=st[("hg", k)][:].rearrange("p c u -> p (c u)").bitcast(BF16),
-            )
-            st[("h", k)] = (hc, hs)
+            hc = work.tile([P, 512], U32, name="hc", tag="hc", align_bytes=64)
+            hs = work.tile([P, 512], U8, name="hs", tag="hs", align_bytes=64)
+            nc.vector.quantize_mx(out=hc[:].bitcast(FP8X4), scales=hs[:], in_=st[("hg", k)])
+            st[("h", k)] = (hc[:], hs[:])
 
         bc = const.tile([P, 8 * 512], U32, name="bc", align_bytes=64)
         bs = const.tile([P, 8 * 512], U8, name="bs", align_bytes=64)
@@ -230,7 +235,7 @@ def tile_languagemsgencoder_pb_kernel(
         def stage1_mm(k, t):
             hc, hs = st[("h", k)]
             s1 = psum.tile([P, 512], F32, name="s1", tag="s1")
-            mx(s1[:], "gc", t, hc[:], hs[:], True, False)
+            mx(s1[:], "gc", t, hc, hs, True, False)
             mx(s1[:], "ga", t, xi_c[:], xi_s[:], False, False)
             mx(s1[:], "gb", t, bc[:, 512 * k : 512 * k + 512], bs[:, 512 * k : 512 * k + 512], False, True)
             st[("s1", k, t)] = s1
@@ -249,27 +254,34 @@ def tile_languagemsgencoder_pb_kernel(
 
         def regroup_rel(k):
             rt = st[("rt", k)]
-            rg = work.tile([P, 512, 4], BF16, name="rg", tag="rg", align_bytes=64)
+            if k < 6:
+                grouped = st[("hr", k)][:, 2048:4096]
+            else:
+                rg = work.tile([P, 2048], BF16, name="rg", tag="rg", align_bytes=64)
+                grouped = rg[:]
             nc.vector.tensor_copy(
-                out=rg[:].rearrange("p (c i) t -> p c t i", i=4),
+                out=grouped.rearrange("p (c i t) -> p c t i", i=4, t=4),
                 in_=rt[:].rearrange("p t (c i) -> p c t i", i=4),
             )
-            st[("rg", k)] = rg
+            st[("rg", k)] = grouped
 
         def quantise_rel(k):
-            rc = work.tile([P, 512], U32, name="rc", tag="rc", align_bytes=64)
-            rs = work.tile([P, 512], U8, name="rs", tag="rs", align_bytes=64)
+            width = 1024 if k < 6 else 512
+            codes = work.tile([P, width], U32, name="qc", tag="qc", bufs=3, align_bytes=64)
+            scales = work.tile([P, width], U8, name="qs", tag="qs", bufs=3, align_bytes=64)
             nc.vector.quantize_mx(
-                out=rc[:].bitcast(FP8X4),
-                scales=rs[:],
-                in_=st[("rg", k)][:].rearrange("p c t -> p (c t)"),
+                out=codes[:].bitcast(FP8X4),
+                scales=scales[:],
+                in_=st[("hr", k)][:] if k < 6 else st[("rg", k)],
             )
-            st[("r", k)] = (rc, rs)
+            if k < 6:
+                st[("h", k + 2)] = (codes[:, 0:512], scales[:, 0:512])
+            st[("r", k)] = (codes[:, width - 512 : width], scales[:, width - 512 : width])
 
         def stage2_mm(k, ct):
             rc, rs = st[("r", k)]
             e = psum.tile([P, 512], F32, name="e", tag="e", bufs=4)
-            mx(e[:], "we", ct, rc[:], rs[:], True, True)
+            mx(e[:], "we", ct, rc, rs, True, True)
             st[("e", k, ct)] = e
 
         def column_max(k, ct):
@@ -442,23 +454,24 @@ def tile_languagemsgencoder_pb_kernel(
             b = bank_at(s + AHEAD_TANH)
             if b is not None:
                 stage1_tanh(b[0], b[1])
-            b = bank_at(s + AHEAD_MAX)
-            if b is not None:
-                column_max(b[0], b[1])
             b = bank_at(s + AHEAD_EXP)
             if b is not None and b[1] == LONG_BANK:
                 subtract_max(b[0], b[1])
+            b = bank_at(s + AHEAD_MAX)
+            if b is not None:
+                column_max(b[0], b[1])
             now = bank_at(s)
             if now is not None:
                 if now[1] == LONG_BANK:
                     sum_exponentials(now[0], now[1])
                 weigh(now[0], now[1])
+            if now is not None:
+                normalise(now[0], now[1], nc.vector if s == N_BANKS - 1 else nc.gpsimd)
             k = unit_at(s, AHEAD_QUANT_REL, 0)
             if k is not None:
                 quantise_rel(k)
-            k = unit_at(s, AHEAD_QUANT_H, 1)
-            if k is not None:
-                quantise_h(k)
+            if s == 4 - AHEAD_QUANT_H:
+                quantise_h(1)
             if s == -AHEAD_SPREAD:
                 spread_xj(1, 8)
             if last:
@@ -474,8 +487,6 @@ def tile_languagemsgencoder_pb_kernel(
                 regroup_rel(k)
             if s == N_BANKS - 2:
                 quantise_weight("go")
-            if now is not None:
-                normalise(now[0], now[1], nc.vector if s == N_BANKS - 1 else nc.gpsimd)
             b = bank_at(s + AHEAD_EXP)
             if b is not None and b[1] == LONG_BANK:
                 long_exponential(b[0], b[1])

@@ -104,6 +104,13 @@ def tile_languagemsgencoder_pb_kernel(
                 }
             )
         )
+        def warm_up(n):
+            for i in range(n):
+                warm = psum.tile([P, 512], F32, name="warm", tag="e", bufs=4)
+                nc.tensor.matmul(
+                    out=warm[:], lhsT=raw["gc"][:, 0, 0:P], rhs=raw["gc"][:, 1, :], start=True, stop=True
+                )
+
         xw = x_sb[:].bitcast(F32)
         xt = psum.tile([P, 2, 2, P], F32, name="xt", tag="tp")
         for u in range(2):
@@ -381,6 +388,11 @@ def tile_languagemsgencoder_pb_kernel(
 
         nxt_sb = const.tile([P, 4, P], F32, name="nxt_sb")
 
+        def keep_warm(k, ct):
+            late = psum.tile([P, 256], F32, name="late", tag="s1")
+            pr = st[("pr", k, ct)][:].rearrange("p j i -> p (j i)")
+            nc.tensor.matmul(out=late[:], lhsT=pr[:, 0:P], rhs=pr[:, 0:256], start=True, stop=True)
+
         def new_x_front():
             nxp = psum.tile([P, 4, P], F32, name="nxp", tag="s1")
             for t in range(4):
@@ -402,6 +414,7 @@ def tile_languagemsgencoder_pb_kernel(
             nc.scalar.copy(out=nxo[:], in_=nxo_ps[:])
             nc.sync.dma_start(out=out_0.flatten_outer_dims(), in_=nxo[:])
 
+        warm_up(3)
         for gp in range(2):
             transpose_half(0, gp)
             copy_out(0, gp)
@@ -423,6 +436,7 @@ def tile_languagemsgencoder_pb_kernel(
         spread_xj(0, 1)
         bt = psum.tile([P, 512], F32, name="bt", tag="tp")
         nc.tensor.transpose(bt[:, 0:P], bf[:], ident[:])
+        warm_up(4)
         nc.scalar.copy(out=bias[:], in_=bt[:, 0:12])
         quantise_weight("we")
         regroup_weight("go", "g")
@@ -442,6 +456,9 @@ def tile_languagemsgencoder_pb_kernel(
                 k = unit_at(s, AHEAD_TRANSPOSE - 2 * gp, 1)
                 if k is not None:
                     transpose_half(k, gp)
+            b = bank_at(s)
+            if b is not None and s >= N_BANKS - 4:
+                keep_warm(b[0], b[1])
             last = s >= N_BANKS
             pair, part = (3, s - N_BANKS) if last else divmod(s - BEHIND_SUM, 8)
             summing = 0 <= pair < (4 if last else 3) and part < 2

@@ -161,9 +161,19 @@ def tile_languagemsgencoder_pb_kernel(
             in_=xg[:].rearrange("p c u -> p (c u)").bitcast(BF16),
         )
         quantise_weight("gc")
-        regroup_weight("ga", "s")
+        xi_c = const.tile([P, 512], U32, name="xi_c", align_bytes=64)
+        xi_s = const.tile([P, 512], U8, name="xi_s", align_bytes=64)
+        nc.vector.tensor_copy(
+            out=xi_c[:].bitcast(I32).rearrange("p (r c) -> p r c", r=4),
+            in_=xc[:].bitcast(I32).unsqueeze(1).to_broadcast([P, 4, P]),
+        )
+        nc.vector.tensor_copy(
+            out=xi_s[:].bitcast(I32).rearrange("p (r c) -> p r c", r=4),
+            in_=xs[:].bitcast(I32).unsqueeze(1).to_broadcast([P, 4, 32]),
+        )
         for r in range(4):
-            nc.gpsimd.tensor_copy(out=x4s[:].rearrange("p (c r) -> p c r", r=4)[:, :, r], in_=xs[:])
+            nc.vector.tensor_copy(out=x4s[:].rearrange("p (c r) -> p c r", r=4)[:, :, r], in_=xs[:])
+        regroup_weight("ga", "s")
         bf = const.tile([P, P], F32, name="bf")
         nc.gpsimd.tensor_copy(out=bf[:], in_=braw[:])
 
@@ -204,7 +214,7 @@ def tile_languagemsgencoder_pb_kernel(
                 .rearrange("p (q c u) -> p q c u", q=2, u=2)
             )
             src = st[("tp", k, gp)][:].rearrange("p q u c -> p q c u")
-            if gp == 0 and k % 2 == 0:
+            if gp == 0 and k in (2, 4, 6):
                 nc.vector.tensor_copy(out=dst, in_=src)
             else:
                 nc.scalar.copy(out=dst, in_=src)
@@ -218,7 +228,7 @@ def tile_languagemsgencoder_pb_kernel(
         bc = const.tile([P, 8 * 512], U32, name="bc", align_bytes=64)
         bs = const.tile([P, 8 * 512], U8, name="bs", align_bytes=64)
 
-        def spread_xj(k0, k1):
+        def spread_xj_codes(k0, k1):
             j0, nj = 4 * k0, 4 * (k1 - k0)
             nc.vector.tensor_copy(
                 out=bc[:, 512 * k0 : 512 * k1].bitcast(I32).rearrange("p (j b i) -> p j b i", j=nj, b=4),
@@ -228,6 +238,9 @@ def tile_languagemsgencoder_pb_kernel(
                 .unsqueeze(3)
                 .to_broadcast([P, nj, 4, 32]),
             )
+
+        def spread_xj_scales(k0, k1):
+            j0, nj = 4 * k0, 4 * (k1 - k0)
             nc.vector.tensor_copy(
                 out=bs[:, 512 * k0 : 512 * k1].bitcast(I32).rearrange("p (j b w) -> p j b w", j=nj, b=4),
                 in_=x4s[:]
@@ -418,22 +431,13 @@ def tile_languagemsgencoder_pb_kernel(
         for gp in range(2):
             transpose_half(0, gp)
             copy_out(0, gp)
-        quantise_weight("ga")
+        spread_xj_codes(0, 1)
         regroup_weight("gb", "v")
+        quantise_weight("ga")
         quantise_h(0)
         quantise_weight("gb")
         regroup_weight("we", "s")
-        xi_c = const.tile([P, 512], U32, name="xi_c", align_bytes=64)
-        xi_s = const.tile([P, 512], U8, name="xi_s", align_bytes=64)
-        nc.vector.tensor_copy(
-            out=xi_c[:].bitcast(I32).rearrange("p (r c) -> p r c", r=4),
-            in_=xc[:].bitcast(I32).unsqueeze(1).to_broadcast([P, 4, P]),
-        )
-        nc.vector.tensor_copy(
-            out=xi_s[:].bitcast(I32).rearrange("p (r c) -> p r c", r=4),
-            in_=xs[:].bitcast(I32).unsqueeze(1).to_broadcast([P, 4, 32]),
-        )
-        spread_xj(0, 1)
+        spread_xj_scales(0, 1)
         bt = psum.tile([P, 512], F32, name="bt", tag="tp")
         nc.tensor.transpose(bt[:, 0:P], bf[:], ident[:])
         warm_up(4)
@@ -457,7 +461,7 @@ def tile_languagemsgencoder_pb_kernel(
                 if k is not None:
                     transpose_half(k, gp)
             b = bank_at(s)
-            if b is not None and s >= N_BANKS - 4:
+            if b is not None and s >= N_BANKS - 10:
                 keep_warm(b[0], b[1])
             last = s >= N_BANKS
             pair, part = (3, s - N_BANKS) if last else divmod(s - BEHIND_SUM, 8)
@@ -490,7 +494,8 @@ def tile_languagemsgencoder_pb_kernel(
             if s == 4 - AHEAD_QUANT_H:
                 quantise_h(1)
             if s == -AHEAD_SPREAD:
-                spread_xj(1, 8)
+                spread_xj_codes(1, 8)
+                spread_xj_scales(1, 8)
             if last:
                 add_up(3, 256 * part, 256 * part + 256)
                 nc.sync.dma_start(

from contextlib import ExitStack

import concourse.mybir as mybir
from concourse.masks import make_identity

F32 = mybir.dt.float32
BF16 = mybir.dt.bfloat16
U32 = mybir.dt.uint32
U8 = mybir.dt.uint8
I32 = mybir.dt.int32
FP8X4 = mybir.dt.float8_e4m3fn_x4
ACT = mybir.ActivationFunctionType
ALU = mybir.AluOpType
AX = mybir.AxisListType

P = 128
FLOPS = 2 * 512 * 512 * (3 * 128 + 2 * 4096)

N_BANKS = 32
LONG_BANK = 0
AHEAD_EXP = 1
AHEAD_MAX = 2
AHEAD_STAGE2 = 3
AHEAD_QUANT_REL = 4
AHEAD_REGROUP = 5
AHEAD_TANH = 9
AHEAD_STAGE1 = 10
AHEAD_SPREAD = 8
AHEAD_QUANT_H = 13
AHEAD_TRANSPOSE = 17
BEHIND_SUM = 11


def bank_at(x):
    if 0 <= x < N_BANKS:
        return divmod(x, 4)
    return None


def tile_languagemsgencoder_pb_kernel(
    tc, node_h, rel_h, W_go, b_go, W_gr, b_gr, W_esa, b_esa, out_0, out_1
):
    nc = tc.nc
    with ExitStack() as ctx:
        const = ctx.enter_context(tc.tile_pool(name="const", bufs=1))
        work = ctx.enter_context(tc.tile_pool(name="work", bufs=2))
        psum = ctx.enter_context(tc.psum_pool(name="psum", bufs=2))

        braw = const.tile([P, P], BF16, name="braw")
        nc.vector.memset(braw[:], 0.0)
        nc.scalar.dma_start(out=braw[0:4, :], in_=b_gr.rearrange("(t p) -> t p", p=P))
        nc.scalar.dma_start(out=braw[4:8, :], in_=b_esa.rearrange("(t p) -> t p", p=P))
        nc.scalar.dma_start(out=braw[8:12, :], in_=b_go.rearrange("(t p) -> t p", p=P))

        x_sb = const.tile([P, 512], BF16, name="x_sb")
        nc.sync.dma_start(out=x_sb[:], in_=node_h.flatten_outer_dims())

        raw = {}

        def load_weight(key, rows, pairs):
            w_raw = const.tile([P, 4, 512], BF16, name="raw_" + key)
            if pairs:
                nc.sync.dma_start(
                    out=w_raw[:].rearrange("p (u e) c -> p u (e c)", u=2),
                    in_=rows.rearrange("(u q e) c -> q u (e c)", u=2, e=2),
                )
            else:
                nc.sync.dma_start(out=w_raw[:], in_=rows.rearrange("(t p) c -> p t c", p=P))
            raw[key] = w_raw

        rel_rows = rel_h.rearrange("b i j k -> (b i) j k")
        rel_raw = []

        def load_rel(k):
            rel_k = const.tile([P, 4, 512], BF16, name="rel_raw%d" % k)
            nc.sync.dma_start(out=rel_k[:], in_=rel_rows[:, 4 * k : 4 * k + 4, :])
            rel_raw.append(rel_k)

        load_weight("gc", W_gr[1024:1536, :], True)
        load_weight("ga", W_gr[0:512, :], True)
        load_rel(0)
        load_weight("gb", W_gr[512:1024, :], True)
        load_weight("we", W_esa, False)
        for k in range(1, 8):
            load_rel(k)
        load_weight("go", W_go, True)

        ident = const.tile([P, P], F32, name="ident")
        make_identity(nc, ident[:])

        xc = const.tile([P, P], U32, name="xc", align_bytes=64)
        xs = const.tile([P, P], U8, name="xs", align_bytes=64)
        x4s = const.tile([P, 512], U8, name="x4s", align_bytes=64)
        nc.vector.memset(xs[:].bitcast(I32), 0)
        nc.vector.memset(x4s[:].bitcast(I32), 0)

        ctx.enter_context(
            tc.manual_schedule(
                engines={
                    mybir.EngineType.PE,
                    mybir.EngineType.Activation,
                    mybir.EngineType.DVE,
                    mybir.EngineType.Pool,
                }
            )
        )
        def warm_up(n):
            for i in range(n):
                warm = psum.tile([P, 512], F32, name="warm", tag="e", bufs=4)
                nc.tensor.matmul(
                    out=warm[:], lhsT=raw["gc"][:, 0, 0:P], rhs=raw["gc"][:, 1, :], start=True, stop=True
                )

        xw = x_sb[:].bitcast(F32)
        xt = psum.tile([P, 2, 2, P], F32, name="xt", tag="tp")
        for u in range(2):
            nc.tensor.transpose(xt[:, 0, u, :], xw[:, 128 * u : 128 * u + 128], ident[:])
        xg = const.tile([P, P, 2], F32, name="xg", align_bytes=64)
        nc.scalar.copy(out=xg[:], in_=xt[:, 0, :, :].rearrange("p u c -> p c u"))

        wc = {}
        ws = {}
        wg = {}

        def regroup_weight(key, engine):
            grouped = work.tile([P, 512, 4], BF16, name="wg", tag="wg", bufs=3, align_bytes=64)
            if engine == "g":
                for h in range(4):
                    nc.gpsimd.tensor_scalar(
                        out=grouped[:, 128 * h : 128 * h + 128, :],
                        in0=raw[key][:, :, 128 * h : 128 * h + 128].rearrange("p t c -> p c t"),
                        scalar1=1.0,
                        scalar2=0.0,
                        op0=ALU.mult,
                        op1=ALU.add,
                    )
            else:
                dst = grouped[:].rearrange("p (c i) t -> p c t i", i=4)
                src = raw[key][:].rearrange("p t (c i) -> p c t i", i=4)
                if engine == "v":
                    nc.vector.tensor_copy(out=dst, in_=src)
                else:
                    nc.scalar.copy(out=dst, in_=src)
            wg[key] = grouped

        def quantise_weight(key):
            codes = const.tile([P, 512], U32, name="c_" + key, align_bytes=64)
            scales = const.tile([P, 512], U8, name="s_" + key, align_bytes=64)
            nc.vector.quantize_mx(
                out=codes[:].bitcast(FP8X4),
                scales=scales[:],
                in_=wg[key][:].rearrange("p c t -> p (c t)"),
            )
            wc[key] = codes
            ws[key] = scales

        regroup_weight("gc", "v")
        nc.vector.quantize_mx(
            out=xc[:].bitcast(FP8X4),
            scales=xs[:],
            in_=xg[:].rearrange("p c u -> p (c u)").bitcast(BF16),
        )
        quantise_weight("gc")
        xi_c = const.tile([P, 512], U32, name="xi_c", align_bytes=64)
        xi_s = const.tile([P, 512], U8, name="xi_s", align_bytes=64)
        nc.vector.tensor_copy(
            out=xi_c[:].bitcast(I32).rearrange("p (r c) -> p r c", r=4),
            in_=xc[:].bitcast(I32).unsqueeze(1).to_broadcast([P, 4, P]),
        )
        nc.vector.tensor_copy(
            out=xi_s[:].bitcast(I32).rearrange("p (r c) -> p r c", r=4),
            in_=xs[:].bitcast(I32).unsqueeze(1).to_broadcast([P, 4, 32]),
        )
        for r in range(4):
            nc.vector.tensor_copy(out=x4s[:].rearrange("p (c r) -> p c r", r=4)[:, :, r], in_=xs[:])
        regroup_weight("ga", "s")
        bf = const.tile([P, P], F32, name="bf")
        nc.gpsimd.tensor_copy(out=bf[:], in_=braw[:])

        def mx(out, key, t, rhs, rhs_scale, start, stop):
            nc.tensor.matmul_mx(
                out=out,
                lhsT=wc[key][:, 128 * t : 128 * t + 128].bitcast(FP8X4),
                lhsT_scale=ws[key][:, 128 * t : 128 * t + 128],
                rhs=rhs.bitcast(FP8X4),
                rhs_scale=rhs_scale,
                start=start,
                stop=stop,
            )

        st = {}

        def transpose_half(k, gp):
            relw = rel_raw[k][:].rearrange("p g k -> p (g k)").bitcast(F32)
            tp = psum.tile([P, 2, 2, P], F32, name="tp", tag="tp")
            for q in range(2):
                for u in range(2):
                    lo = 256 * (2 * gp + q) + 128 * u
                    nc.tensor.transpose(tp[:, q, u, :], relw[:, lo : lo + 128], ident[:])
            st[("tp", k, gp)] = tp

        def copy_out(k, gp):
            if k < 2:
                if gp == 0:
                    hg_new = work.tile([P, 2048], BF16, name="hg", tag="hg", align_bytes=64)
                    st[("hg", k)] = hg_new[:]
            elif gp == 0:
                hr_new = work.tile([P, 4096], BF16, name="hr", tag="hr", bufs=3, align_bytes=64)
                st[("hr", k - 2)] = hr_new
                st[("hg", k)] = hr_new[:, 0:2048]
            dst = (
                st[("hg", k)][:, 1024 * gp : 1024 * gp + 1024]
                .bitcast(F32)
                .rearrange("p (q c u) -> p q c u", q=2, u=2)
            )
            src = st[("tp", k, gp)][:].rearrange("p q u c -> p q c u")
            if gp == 0 and k in (2, 4, 6):
                nc.vector.tensor_copy(out=dst, in_=src)
            else:
                nc.scalar.copy(out=dst, in_=src)

        def quantise_h(k):
            hc = work.tile([P, 512], U32, name="hc", tag="hc", align_bytes=64)
            hs = work.tile([P, 512], U8, name="hs", tag="hs", align_bytes=64)
            nc.vector.quantize_mx(out=hc[:].bitcast(FP8X4), scales=hs[:], in_=st[("hg", k)])
            st[("h", k)] = (hc[:], hs[:])

        bc = const.tile([P, 8 * 512], U32, name="bc", align_bytes=64)
        bs = const.tile([P, 8 * 512], U8, name="bs", align_bytes=64)

        def spread_xj_codes(k0, k1):
            j0, nj = 4 * k0, 4 * (k1 - k0)
            nc.vector.tensor_copy(
                out=bc[:, 512 * k0 : 512 * k1].bitcast(I32).rearrange("p (j b i) -> p j b i", j=nj, b=4),
                in_=xc[:]
                .bitcast(I32)
                .rearrange("p (b j) -> p j b", b=4)[:, j0 : j0 + nj, :]
                .unsqueeze(3)
                .to_broadcast([P, nj, 4, 32]),
            )

        def spread_xj_scales(k0, k1):
            j0, nj = 4 * k0, 4 * (k1 - k0)
            nc.vector.tensor_copy(
                out=bs[:, 512 * k0 : 512 * k1].bitcast(I32).rearrange("p (j b w) -> p j b w", j=nj, b=4),
                in_=x4s[:]
                .bitcast(I32)
                .rearrange("p (b j) -> p j b", b=4)[:, j0 : j0 + nj, :]
                .unsqueeze(3)
                .to_broadcast([P, nj, 4, 8]),
            )

        bias = const.tile([P, 12], F32, name="bias")

        def stage1_mm(k, t):
            hc, hs = st[("h", k)]
            s1 = psum.tile([P, 512], F32, name="s1", tag="s1")
            mx(s1[:], "gc", t, hc, hs, True, False)
            mx(s1[:], "ga", t, xi_c[:], xi_s[:], False, False)
            mx(s1[:], "gb", t, bc[:, 512 * k : 512 * k + 512], bs[:, 512 * k : 512 * k + 512], False, True)
            st[("s1", k, t)] = s1

        def stage1_tanh(k, t):
            if t == 0:
                rt_new = work.tile([P, 4, 512], BF16, name="rt", tag="rt")
                st[("rt", k)] = rt_new
            nc.scalar.activation(
                out=st[("rt", k)][:, t, :],
                in_=st[("s1", k, t)][:],
                func=ACT.Tanh,
                bias=bias[:, t : t + 1],
                scale=1.0,
            )

        def regroup_rel(k):
            rt = st[("rt", k)]
            if k < 6:
                grouped = st[("hr", k)][:, 2048:4096]
            else:
                rg = work.tile([P, 2048], BF16, name="rg", tag="rg", align_bytes=64)
                grouped = rg[:]
            nc.vector.tensor_copy(
                out=grouped.rearrange("p (c i t) -> p c t i", i=4, t=4),
                in_=rt[:].rearrange("p t (c i) -> p c t i", i=4),
            )
            st[("rg", k)] = grouped

        def quantise_rel(k):
            width = 1024 if k < 6 else 512
            codes = work.tile([P, width], U32, name="qc", tag="qc", bufs=3, align_bytes=64)
            scales = work.tile([P, width], U8, name="qs", tag="qs", bufs=3, align_bytes=64)
            nc.vector.quantize_mx(
                out=codes[:].bitcast(FP8X4),
                scales=scales[:],
                in_=st[("hr", k)][:] if k < 6 else st[("rg", k)],
            )
            if k < 6:
                st[("h", k + 2)] = (codes[:, 0:512], scales[:, 0:512])
            st[("r", k)] = (codes[:, width - 512 : width], scales[:, width - 512 : width])

        def stage2_mm(k, ct):
            rc, rs = st[("r", k)]
            e = psum.tile([P, 512], F32, name="e", tag="e", bufs=4)
            mx(e[:], "we", ct, rc, rs, True, True)
            st[("e", k, ct)] = e

        def column_max(k, ct):
            e3 = st[("e", k, ct)][:].rearrange("p (j i) -> p j i", i=32)
            negm = work.tile([P, 16], F32, name="negm", tag="negm", bufs=4)
            nc.vector.tensor_reduce(out=negm[:], in_=e3, axis=AX.X, op=ALU.max, negate=True)
            st[("negm", k, ct)] = negm

        def subtract_max(k, ct):
            e3 = st[("e", k, ct)][:].rearrange("p (j i) -> p j i", i=32)
            d = work.tile([P, 16, 32], F32, name="d", tag="d", bufs=2)
            nc.vector.tensor_tensor(
                out=d[:],
                in0=e3,
                in1=st[("negm", k, ct)][:].unsqueeze(2).to_broadcast([P, 16, 32]),
                op=ALU.add,
            )
            st[("d", k, ct)] = d

        def short_exponentials(k, ct):
            pr = work.tile([P, 16, 32], F32, name="pr", tag="pr", bufs=4)
            st[("pr", k, ct)] = pr
            e3 = st[("e", k, ct)][:].rearrange("p (j i) -> p j i", i=32)
            negm = st[("negm", k, ct)]
            z = work.tile([P, 16], F32, name="zs", tag="zs", bufs=4)
            for j in range(16):
                nc.scalar.activation(
                    out=pr[:, j, :],
                    in_=e3[:, j, :],
                    func=ACT.Exp,
                    bias=negm[:, j : j + 1],
                    scale=1.0,
                    accum_out=z[:, j : j + 1],
                )
            st[("z", k, ct)] = z

        def long_exponential(k, ct):
            pr = work.tile([P, 16, 32], F32, name="pr", tag="pr", bufs=4)
            st[("pr", k, ct)] = pr
            nc.scalar.activation(out=pr[:], in_=st[("d", k, ct)][:], func=ACT.Exp)

        def sum_exponentials(k, ct):
            z = work.tile([P, 16], F32, name="zv", tag="zv", bufs=2)
            nc.vector.tensor_reduce(out=z[:], in_=st[("pr", k, ct)][:], axis=AX.X, op=ALU.add)
            st[("z", k, ct)] = z

        def weigh(k, ct):
            y = work.tile([P, 16, 32], F32, name="y", tag="y", bufs=5)
            nc.vector.scalar_tensor_tensor(
                out=y[:].rearrange("p j i -> p (j i)"),
                in0=st[("e", k, ct)][:],
                scalar=bias[:, 4 + ct : 5 + ct],
                in1=st[("pr", k, ct)][:].rearrange("p j i -> p (j i)"),
                op0=ALU.add,
                op1=ALU.mult,
            )
            st[("y", k, ct)] = y

        def normalise(k, ct, engine):
            rz = work.tile([P, 16], F32, name="rz", tag="rz", bufs=4)
            nc.vector.reciprocal(out=rz[:], in_=st[("z", k, ct)][:])
            u = work.tile([P, 16, 32], F32, name="u", tag="u", bufs=16)
            engine.tensor_tensor(
                out=u[:],
                in0=st[("y", k, ct)][:],
                in1=rz[:].unsqueeze(2).to_broadcast([P, 16, 32]),
                op=ALU.mult,
            )
            st[("u", k, ct)] = u

        ro = const.tile([P, 512], F32, name="ro")

        def sum_over_j(pair, ct):
            if ct == 0:
                acc_new = psum.tile([P, 512], F32, name="acc", tag="tp")
                st[("acc", pair)] = acc_new
            acc = st[("acc", pair)]
            for n in range(8):
                h, jj = divmod(n, 4)
                nc.tensor.matmul(
                    out=acc[:, 128 * ct : 128 * ct + 128],
                    lhsT=st[("u", 2 * pair + h, ct)][:].rearrange("p j i -> p (j i)")[
                        :, 128 * jj : 128 * jj + 128
                    ],
                    rhs=ident[:],
                    start=(n == 0),
                    stop=(n == 7),
                    is_transpose=True,
                )

        def add_up(pair, lo, hi):
            acc = st[("acc", pair)]
            if pair == 0:
                nc.vector.tensor_copy(out=ro[:, lo:hi], in_=acc[:, lo:hi])
            else:
                nc.vector.tensor_tensor(out=ro[:, lo:hi], in0=acc[:, lo:hi], in1=ro[:, lo:hi], op=ALU.add)

        nxt_sb = const.tile([P, 4, P], F32, name="nxt_sb")

        def keep_warm(k, ct):
            late = psum.tile([P, 256], F32, name="late", tag="s1")
            pr = st[("pr", k, ct)][:].rearrange("p j i -> p (j i)")
            nc.tensor.matmul(out=late[:], lhsT=pr[:, 0:P], rhs=pr[:, 0:256], start=True, stop=True)

        def new_x_front():
            nxp = psum.tile([P, 4, P], F32, name="nxp", tag="s1")
            for t in range(4):
                mx(nxp[:, t, :], "go", t, xc[:], xs[:], True, True)
            for t in range(4):
                nc.scalar.activation(
                    out=nxt_sb[:, t, :],
                    in_=nxp[:, t, :],
                    func=ACT.Tanh,
                    bias=bias[:, 8 + t : 9 + t],
                    scale=1.0,
                )

        def new_x_back():
            nxo_ps = psum.tile([P, 512], F32, name="nxo_ps", tag="e", bufs=4)
            for t in range(4):
                nc.tensor.transpose(nxo_ps[:, 128 * t : 128 * t + 128], nxt_sb[:, t, :], ident[:])
            nxo = const.tile([P, 512], F32, name="nxo")
            nc.scalar.copy(out=nxo[:], in_=nxo_ps[:])
            nc.sync.dma_start(out=out_0.flatten_outer_dims(), in_=nxo[:])

        warm_up(3)
        for gp in range(2):
            transpose_half(0, gp)
            copy_out(0, gp)
        spread_xj_codes(0, 1)
        regroup_weight("gb", "v")
        quantise_weight("ga")
        quantise_h(0)
        quantise_weight("gb")
        regroup_weight("we", "s")
        spread_xj_scales(0, 1)
        bt = psum.tile([P, 512], F32, name="bt", tag="tp")
        nc.tensor.transpose(bt[:, 0:P], bf[:], ident[:])
        warm_up(4)
        nc.scalar.copy(out=bias[:], in_=bt[:, 0:12])
        quantise_weight("we")
        regroup_weight("go", "g")

        def unit_at(s, ahead, first):
            k, part = divmod(s + ahead, 4)
            return k if part == 0 and first <= k < 8 else None

        for s in range(-AHEAD_TRANSPOSE, N_BANKS + 2):
            b = bank_at(s + AHEAD_STAGE2)
            if b is not None:
                stage2_mm(b[0], b[1])
            b = bank_at(s + AHEAD_STAGE1)
            if b is not None:
                stage1_mm(b[0], b[1])
            for gp in range(2):
                k = unit_at(s, AHEAD_TRANSPOSE - 2 * gp, 1)
                if k is not None:
                    transpose_half(k, gp)
            b = bank_at(s)
            if b is not None and s >= N_BANKS - 10:
                keep_warm(b[0], b[1])
            last = s >= N_BANKS
            pair, part = (3, s - N_BANKS) if last else divmod(s - BEHIND_SUM, 8)
            summing = 0 <= pair < (4 if last else 3) and part < 2
            if summing:
                sum_over_j(pair, 2 * part)
                sum_over_j(pair, 2 * part + 1)
            b = bank_at(s + AHEAD_EXP)
            if b is not None and b[1] != LONG_BANK:
                short_exponentials(b[0], b[1])
            b = bank_at(s + AHEAD_TANH)
            if b is not None:
                stage1_tanh(b[0], b[1])
            b = bank_at(s + AHEAD_EXP)
            if b is not None and b[1] == LONG_BANK:
                subtract_max(b[0], b[1])
            b = bank_at(s + AHEAD_MAX)
            if b is not None:
                column_max(b[0], b[1])
            now = bank_at(s)
            if now is not None:
                if now[1] == LONG_BANK:
                    sum_exponentials(now[0], now[1])
                weigh(now[0], now[1])
            if now is not None:
                normalise(now[0], now[1], nc.vector if s == N_BANKS - 1 else nc.gpsimd)
            k = unit_at(s, AHEAD_QUANT_REL, 0)
            if k is not None:
                quantise_rel(k)
            if s == 4 - AHEAD_QUANT_H:
                quantise_h(1)
            if s == -AHEAD_SPREAD:
                spread_xj_codes(1, 8)
                spread_xj_scales(1, 8)
            if last:
                add_up(3, 256 * part, 256 * part + 256)
                nc.sync.dma_start(
                    out=out_1.flatten_outer_dims()[:, 256 * part : 256 * part + 256],
                    in_=ro[:, 256 * part : 256 * part + 256],
                )
            elif 0 <= pair < 3 and part == 2:
                add_up(pair, 0, 512)
            k = unit_at(s, AHEAD_REGROUP, 0)
            if k is not None:
                regroup_rel(k)
            if s == N_BANKS - 2:
                quantise_weight("go")
            b = bank_at(s + AHEAD_EXP)
            if b is not None and b[1] == LONG_BANK:
                long_exponential(b[0], b[1])
            for gp in range(2):
                k = unit_at(s, AHEAD_TRANSPOSE - 1 - 2 * gp, 1)
                if k is not None:
                    copy_out(k, gp)
            if s == N_BANKS - 1:
                new_x_front()
            if s == N_BANKS:
                new_x_back()
